import numpy as np
import ml_dtypes


def mxq(x, axis, fmt="e4m3"):
    dtype, down = {"e4m3": (ml_dtypes.float8_e4m3fn, 7), "e5m2": (ml_dtypes.float8_e5m2, 14)}[fmt]
    v = np.moveaxis(np.asarray(x, np.float32).astype(ml_dtypes.bfloat16).astype(np.float64), axis, -1)
    blocks = v.reshape(v.shape[:-1] + (-1, 32))
    amax = np.abs(blocks).max(-1, keepdims=True)
    byte = np.maximum(np.where(amax > 0, np.frexp(amax)[1] - 1 + 127, 0) - down, 1)
    scale = np.exp2(byte - 127.0)
    codes = (blocks / scale).astype(np.float32).astype(dtype).astype(np.float64)
    return np.moveaxis((codes * scale).reshape(v.shape), -1, axis)


WIDE = False


def mx_kscale(k):
    if not WIDE:
        return np.ones(k)
    levels = np.array([10, -10, 5, -5, 0])
    if k % 512:
        return np.exp2(np.random.permutation(np.resize(levels, k // 32))).repeat(32)
    a = np.empty((k // 512, 16))
    for p in range(k // 512):
        a[p, :8] = np.random.permutation(np.resize(levels, 8))
        for g in range(8):
            far = levels[np.abs(levels - a[p, g]) >= 10]
            a[p, g + 8] = far[np.random.randint(len(far))]
    return np.exp2(a.ravel()).repeat(32)


BF16 = ml_dtypes.bfloat16


def bf(x):
    return np.asarray(x, np.float32).astype(BF16)


def f64(x):
    return np.asarray(x).astype(np.float64)


B, F, D = 256, 128, 24
K = F * D
LN_EPS = 1e-5


def layernorm(x, w, b):
    mu = x.mean(-1, keepdims=True)
    var = ((x - mu) ** 2).mean(-1, keepdims=True)
    return (x - mu) / np.sqrt(var + LN_EPS) * w + b


def draw0():
    s = mx_kscale(K)
    sf = s.reshape(F, D)
    a = np.random.standard_normal((B, F, D))
    c = np.random.standard_normal((B, F, D))
    return {"r": bf(np.random.standard_normal((B, F, D)) * sf),
            "p": bf(np.random.standard_normal((B, F, D)) * sf),
            "log_lam": bf(0.5 * np.log(a ** 2 + c ** 2 + 1e-8)),
            "theta": bf(np.random.uniform(-np.pi, np.pi, (B, F, D))),
            "inter_orders": bf(np.random.standard_normal((F, F)) / np.sqrt(F)),
            "im_w": bf(np.random.standard_normal((K, K)) / np.sqrt(K) / s[:, None]),
            "im_b": bf(np.random.standard_normal(K) * 0.3),
            "bias_lam": bf(np.random.standard_normal((1, D, F)) * 0.3),
            "bias_theta": bf(np.random.standard_normal((1, D, F)) * 0.3),
            "norm_r_w": bf(1.0 + 0.2 * np.random.standard_normal(D)),
            "norm_r_b": bf(0.2 * np.random.standard_normal(D)),
            "norm_p_w": bf(1.0 + 0.2 * np.random.standard_normal(D)),
            "norm_p_b": bf(0.2 * np.random.standard_normal(D))}


def core(r, p, log_lam, theta, inter_orders, im_w, im_b, bias_lam, bias_theta, norm_r_w, norm_r_b, norm_p_w, norm_p_b):
    io = f64(inter_orders)
    lam_t = np.swapaxes(f64(log_lam), -2, -1) @ io + f64(bias_lam)
    theta_t = np.swapaxes(f64(theta), -2, -1) @ io + f64(bias_theta)
    lam = np.swapaxes(np.exp(lam_t), -2, -1)
    th = np.swapaxes(theta_t, -2, -1)
    wq = mxq(f64(im_w), 0, "e4m3")
    r_lin = np.maximum((mxq(f64(r).reshape(B, K), 1, "e4m3") @ wq) + f64(im_b), 0.0).reshape(B, F, D)
    p_lin = np.maximum((mxq(f64(p).reshape(B, K), 1, "e4m3") @ wq) + f64(im_b), 0.0).reshape(B, F, D)
    o_r = r_lin + lam * np.cos(th)
    o_p = p_lin + lam * np.sin(th)
    return (layernorm(o_r, f64(norm_r_w), f64(norm_r_b)), layernorm(o_p, f64(norm_p_w), f64(norm_p_b)))


def e4m3fn_bytes(y):
    return np.clip(np.asarray(y, np.float64), -448.0, 448.0).astype(np.float32).astype(ml_dtypes.float8_e4m3fn).view(np.uint8)


def e4m3fn_values(b):
    return np.asarray(b, np.uint8).view(ml_dtypes.float8_e4m3fn).astype(np.float64)


def setup_inputs():
    d = draw0()
    x0 = np.asarray(d['im_w']).astype(np.float64)
    s = (np.max(np.abs(x0), axis=(1,), keepdims=True) / 448.0).astype(np.float32)
    out = {}
    for k, v in d.items():
        if k == 'im_w':
            out['im_w_bytes'] = e4m3fn_bytes(x0 / s.astype(np.float64))
            out['im_w_scale'] = s
        else:
            out[k] = v
    return out


def reference(r, p, log_lam, theta, inter_orders, im_w_bytes, im_w_scale, im_b, bias_lam, bias_theta, norm_r_w, norm_r_b, norm_p_w, norm_p_b):
    return core(r, p, log_lam, theta, inter_orders, e4m3fn_values(im_w_bytes) * im_w_scale.astype(np.float64), im_b, bias_lam, bias_theta, norm_r_w, norm_r_b, norm_p_w, norm_p_b)

@@ -1,0 +1,290 @@
+from contextlib import ExitStack
+import math
+
+import concourse.mybir as mybir
+from concourse.masks import make_identity
+
+B, F, D = 256, 128, 24
+K = F * D
+LN_EPS = 1e-5
+
+F32 = mybir.dt.float32
+BF16 = mybir.dt.bfloat16
+I32 = mybir.dt.int32
+U32 = mybir.dt.uint32
+U8 = mybir.dt.uint8
+FP8 = mybir.dt.float8_e4m3fn
+FP8X4 = mybir.dt.float8_e4m3fn_x4
+ALU = mybir.AluOpType
+ACT = mybir.ActivationFunctionType
+AX = mybir.AxisListType
+
+P = 128
+PASSES = K // 512
+NC = 512
+CHUNKS = K // NC
+MT = 4
+NT = K // P
+UT = 3
+UG = UT * P // D
+TWO_PI = 2.0 * math.pi
+SB_UNITS = {(j, 3) for j in range(1, 6)}
+Y4_ON_VECTOR = ()
+
+FLOPS = 2 * (2 * B) * K * K + 2 * 2 * B * D * F * F
+
+
+def tile_eulerinteractionlayer_pa_kernel(
+    tc, r, p, log_lam, theta, inter_orders, im_w_bytes, im_w_scale, im_b,
+    bias_lam, bias_theta, norm_r_w, norm_r_b, norm_p_w, norm_p_b, out_0, out_1,
+):
+    nc = tc.nc
+    with ExitStack() as ctx:
+        const = ctx.enter_context(tc.tile_pool(name="const", bufs=1))
+        rawp = ctx.enter_context(tc.tile_pool(name="rawp", bufs=3))
+        xgp = ctx.enter_context(tc.tile_pool(name="xgp", bufs=2))
+        ltp = ctx.enter_context(tc.tile_pool(name="ltp", bufs=2))
+        ktp = ctx.enter_context(tc.tile_pool(name="ktp", bufs=2))
+        wrawp = ctx.enter_context(tc.tile_pool(name="wrawp", bufs=8))
+        plp = ctx.enter_context(tc.tile_pool(name="plp", bufs=3))
+        grp_pool = ctx.enter_context(tc.tile_pool(name="grpp", bufs=3))
+        wcp = ctx.enter_context(tc.tile_pool(name="wcp", bufs=2))
+        scr = ctx.enter_context(tc.tile_pool(name="scr", bufs=3))
+        atp = ctx.enter_context(tc.tile_pool(name="atp", bufs=3))
+        stp = ctx.enter_context(tc.tile_pool(name="stp", bufs=2))
+        psum = ctx.enter_context(tc.psum_pool(name="psum", bufs=2))
+
+        wview = im_w_bytes.rearrange("(g q t) n -> g q t n", q=P, t=4)
+        outv = [o.rearrange("(t q) g d -> q t (g d)", q=P) for o in (out_0, out_1)]
+        r2 = r.rearrange("b f d -> b (f d)")
+        p2 = p.rearrange("b f d -> b (f d)")
+        xsrc = [r2[0:P, :], r2[P:2 * P, :], p2[0:P, :], p2[P:2 * P, :]]
+
+        def load_w(j, g):
+            wraw = wrawp.tile([P, 4, NC], U8, name="wraw", tag="wraw")
+            nc.sync.dma_start(out=wraw[:], in_=wview[g][:, :, j * NC:(j + 1) * NC])
+            return wraw
+
+        wsc = const.tile([P, PASSES, 4], F32, name="wsc")
+        nc.sync.dma_start(out=wsc[:], in_=im_w_scale.rearrange("(g q t) o -> q g (t o)", q=P, t=4))
+        first_w = []
+        xraws = []
+        for g in range(PASSES):
+            first_w.append(load_w(0, g))
+            if g < 3:
+                xraw = rawp.tile([P, K], BF16, name="xraw", tag="raw")
+                nc.sync.dma_start(out=xraw[:], in_=xsrc[g])
+                xraws.append(xraw)
+
+        ident_f = const.tile([P, P], F32, name="ident_f")
+        make_identity(nc, ident_f[:])
+        ident_b = const.tile([P, P], BF16, name="ident_b")
+        make_identity(nc, ident_b[:])
+        io_sb = const.tile([P, P], BF16, name="io_sb")
+        bias_sb = const.tile([P, 2, P], BF16, name="bias_sb")
+        nc.vector.memset(bias_sb[:], 0.0)
+        imb_rows = const.tile([P, P], BF16, name="imb_rows")
+        nc.vector.memset(imb_rows[:], 0.0)
+        imb_col = const.tile([P, NT], F32, name="imb_col")
+        lnw = const.tile([P, 4, 32], BF16, name="lnw")
+        wcol = const.tile([P, UT, 4], F32, name="wcol")
+        xc = const.tile([P, PASSES, MT * P], U32, name="xc", align_bytes=64)
+        xs = const.tile([P, PASSES, MT * P], U8, name="xs", align_bytes=64)
+        pol = const.tile([P, MT, K], F32, name="pol")
+        polv = pol[:].rearrange("q m (g d) -> q m g d", d=D)
+
+        tst = const.tile([P, 1], F32, name="tst")
+        nc.vector.memset(tst[:], 0.75)
+        tsti = const.tile([P, 1], I32, name="tsti")
+        nc.vector.tensor_copy(out=tsti[:], in_=tst[:])
+        tstf = const.tile([P, 1], F32, name="tstf")
+        nc.vector.tensor_copy(out=tstf[:], in_=tsti[:])
+        tstz = const.tile([P, 1], F32, name="tstz")
+        nc.vector.tensor_scalar(out=tstz[:], in0=tstf[:], scalar1=-1.0, scalar2=None, op0=ALU.add)
+
+        for m in range(MT):
+            if m < 3:
+                xraw = xraws[m]
+            else:
+                xraw = rawp.tile([P, K], BF16, name="xraw", tag="raw")
+                nc.sync.dma_start(out=xraw[:], in_=xsrc[m])
+            words = xraw[:].bitcast(F32)
+            for h in range(PASSES // 2):
+                xt = psum.tile([P, 2, 2, P], F32, name="xt", tag="tT")
+                for gi in range(2):
+                    g = 2 * h + gi
+                    for u in range(2):
+                        nc.tensor.transpose(xt[:, gi, u, :], words[:, 256 * g + u:256 * (g + 1):2], ident_f[:])
+                xg = xgp.tile([P, 2, P, 4], BF16, name="xg", tag="xg", align_bytes=64)
+                nc.vector.tensor_copy(
+                    out=xg[:].rearrange("q a r t -> q (a r t)").bitcast(F32).rearrange("q (a r u) -> q a r u", a=2, u=2),
+                    in_=xt[:].rearrange("q a u r -> q a r u"),
+                )
+                for gi in range(2):
+                    g = 2 * h + gi
+                    nc.vector.quantize_mx(
+                        out=xc[:, g, m * P:(m + 1) * P].bitcast(FP8X4),
+                        scales=xs[:, g, m * P:(m + 1) * P],
+                        in_=xg[:, gi, :, :].rearrange("q r t -> q (r t)"),
+                    )
+
+        def prep(j, raws):
+            wc = wcp.tile([P, PASSES, NC], U32, name="wc", tag="wc", align_bytes=64)
+            ws = wcp.tile([P, PASSES, NC], U8, name="ws", tag="ws", align_bytes=64)
+            for g in range(PASSES):
+                wraw = raws[g] if raws else load_w(j, g)
+                planes = plp.tile([P, 4, NC], BF16, name="planes", tag="planes")
+                for t in range(4):
+                    nc.scalar.activation(out=planes[:, t, :], in_=wraw[:, t, :].bitcast(FP8), func=ACT.Copy,
+                                         scale=wsc[:, g, t:t + 1])
+                grp = grp_pool.tile([P, NC, 4], BF16, name="grp", tag="grp", align_bytes=64)
+                if (j, g) in SB_UNITS:
+                    nc.scalar.copy(out=grp[:], in_=planes[:].rearrange("q t n -> q n t"))
+                else:
+                    nc.vector.tensor_copy(out=grp[:], in_=planes[:].rearrange("q t n -> q n t"))
+                nc.vector.quantize_mx(out=wc[:, g, :].bitcast(FP8X4), scales=ws[:, g, :],
+                                      in_=grp[:].rearrange("q n t -> q (n t)"))
+            return wc, ws
+
+        def linear_tile(i, wc, ws):
+            li = i % (NC // P)
+            cols = slice(li * P, (li + 1) * P)
+            acc = psum.tile([P, MT * P], F32, name="acc", tag="acc")
+            for g in range(PASSES):
+                nc.tensor.matmul_mx(
+                    out=acc[:],
+                    lhsT=wc[:, g, cols].bitcast(FP8X4), lhsT_scale=ws[:, g, cols],
+                    rhs=xc[:, g, :].bitcast(FP8X4), rhs_scale=xs[:, g, :],
+                    start=(g == 0), stop=(g == PASSES - 1),
+                )
+            a_t = atp.tile([P, MT * P], F32, name="a_t", tag="a_t")
+            nc.scalar.activation(out=a_t[:], in_=acc[:], func=ACT.Relu, bias=imb_col[:, i:i + 1])
+            a4 = psum.tile([P, MT, P], F32, name="a4", tag="a4")
+            for m in range(MT):
+                nc.tensor.transpose(a4[:, m, :], a_t[:, m * P:(m + 1) * P], ident_f[:])
+            ncols = slice(i * P, (i + 1) * P)
+            nc.vector.tensor_tensor(out=pol[:, :, ncols], in0=a4[:], in1=pol[:, :, ncols], op=ALU.add)
+
+        def normalise(u):
+            g0 = u * UG
+            o = polv[:, :, g0:g0 + UG, :]
+            s1 = stp.tile([P, MT, UG], F32, name="s1", tag="s1")
+            nc.vector.tensor_reduce(out=s1[:], in_=o, axis=AX.X, op=ALU.add)
+            nc.vector.scalar_tensor_tensor(out=o, in0=s1[:].unsqueeze(3).to_broadcast([P, MT, UG, D]),
+                                           scalar=-1.0 / D, in1=o, op0=ALU.mult, op1=ALU.add)
+            sq = scr.tile([P, MT, UG, D], F32, name="sq", tag="scr")
+            nc.scalar.activation(out=sq[:], in_=o, func=ACT.Square)
+            s2 = stp.tile([P, MT, UG], F32, name="s2", tag="s2")
+            nc.vector.tensor_reduce(out=s2[:], in_=sq[:], axis=AX.X, op=ALU.add)
+            sd = stp.tile([P, MT, UG], F32, name="sd", tag="sd")
+            nc.scalar.activation(out=sd[:], in_=s2[:], func=ACT.Sqrt, scale=1.0 / D, bias=LN_EPS)
+            rho = stp.tile([P, MT, UG], F32, name="rho", tag="rho")
+            nc.vector.reciprocal(out=rho[:], in_=sd[:])
+            nc.vector.tensor_tensor(out=o, in0=o, in1=rho[:].unsqueeze(3).to_broadcast([P, MT, UG, D]),
+                                    op=ALU.mult)
+
+        def affine_tile(i):
+            ncols = slice(i * P, (i + 1) * P)
+            t_t = psum.tile([P, MT * P], F32, name="t_t", tag="tT")
+            for m in range(MT):
+                nc.tensor.transpose(t_t[:, m * P:(m + 1) * P], pol[:, m, ncols], ident_f[:])
+            y_t = atp.tile([P, MT * P], F32, name="y_t", tag="y_t")
+            for rp in range(2):
+                half = slice(rp * 2 * P, (rp + 1) * 2 * P)
+                nc.scalar.activation(out=y_t[:, half], in_=t_t[:, half], func=ACT.Identity,
+                                     scale=wcol[:, i % UT, 2 * rp:2 * rp + 1],
+                                     bias=wcol[:, i % UT, 2 * rp + 1:2 * rp + 2])
+            y4 = psum.tile([P, MT, P], F32, name="y4", tag="y4")
+            for m in range(MT):
+                nc.tensor.transpose(y4[:, m, :], y_t[:, m * P:(m + 1) * P], ident_f[:])
+            if i in Y4_ON_VECTOR:
+                nc.vector.tensor_copy(out=pol[:, :, ncols], in_=y4[:])
+            else:
+                nc.scalar.copy(out=pol[:, :, ncols], in_=y4[:])
+
+        def finish(u):
+            normalise(u)
+            for i in range(UT * u, UT * (u + 1)):
+                affine_tile(i)
+            ucols = slice(u * UT * P, (u + 1) * UT * P)
+            for rp in range(2):
+                nc.sync.dma_start(out=outv[rp][:, :, ucols], in_=pol[:, 2 * rp:2 * rp + 2, ucols])
+
+        codes = prep(0, first_w)
+
+        nc.sync.dma_start(out=io_sb[:], in_=inter_orders)
+        nc.sync.dma_start(out=bias_sb[0:D, 0, :], in_=bias_lam.rearrange("o d g -> (o d) g"))
+        nc.sync.dma_start(out=bias_sb[0:D, 1, :], in_=bias_theta.rearrange("o d g -> (o d) g"))
+        nc.sync.dma_start(out=imb_rows[0:NT, :], in_=im_b.rearrange("(i q) -> i q", q=P))
+        for k, v in enumerate((norm_r_w, norm_r_b, norm_p_w, norm_p_b)):
+            nc.sync.dma_start(out=lnw[:, k, 0:D], in_=v.partition_broadcast(P))
+
+        lsrc = [log_lam.rearrange("b f d -> b (f d)"), theta.rearrange("b f d -> b (f d)")]
+        lams = []
+        for x in range(2):
+            for bt in range(2):
+                lraw = rawp.tile([P, K], BF16, name="lraw", tag="raw")
+                nc.sync.dma_start(out=lraw[:], in_=lsrc[x][bt * P:(bt + 1) * P, :])
+                lw = lraw[:].bitcast(F32)
+                lt = ltp.tile([P, D // 2, P], F32, name="lt", tag="lt")
+                for q in range(3):
+                    tpb = psum.tile([P, 4, P], F32, name="tpb", tag="tT")
+                    for i in range(4):
+                        nc.tensor.transpose(tpb[:, i, :], lw[:, 4 * q + i:K // 2:D // 2], ident_f[:])
+                    nc.vector.tensor_copy(out=lt[:, 4 * q:4 * q + 4, :], in_=tpb[:])
+                ltb = lt[:].rearrange("q a b -> q (a b)").bitcast(BF16).rearrange("q (a b e) -> q a b e", a=D // 2, e=2)
+                if x == 0:
+                    lam = scr.tile([P, F, D], F32, name="lam", tag="scr")
+                    lams.append(lam)
+                for dq in range(D // 4):
+                    pp = psum.tile([P, 4, P], F32, name="pp", tag="y4")
+                    for i in range(4):
+                        d = 4 * dq + i
+                        nc.tensor.matmul(out=pp[:, i, :], lhsT=ltb[:, d // 2, :, d % 2], rhs=io_sb[:],
+                                         start=True, stop=False)
+                        nc.tensor.matmul(out=pp[:, i, :], lhsT=ident_b[:, d:d + 1].to_broadcast([P, P]),
+                                         rhs=bias_sb[:, x, :], start=False, stop=True)
+                    ppv = pp[:].rearrange("q i g -> q g i")
+                    if x == 0:
+                        nc.scalar.activation(out=lam[:, :, 4 * dq:4 * dq + 4], in_=ppv, func=ACT.Exp)
+                    else:
+                        kt = ktp.tile([P, 4, P], I32, name="kt", tag="kt")
+                        nc.vector.tensor_scalar(out=kt[:], in0=pp[:], scalar1=1.0 / TWO_PI, scalar2=None, op0=ALU.mult)
+                        nc.vector.scalar_tensor_tensor(out=polv[:, bt, :, 4 * dq:4 * dq + 4],
+                                                       in0=kt[:].rearrange("q i g -> q g i"), scalar=-TWO_PI,
+                                                       in1=ppv, op0=ALU.mult, op1=ALU.add)
+
+        imb_ps = psum.tile([P, P], BF16, name="imb_ps", tag="a4")
+        nc.tensor.transpose(imb_ps[:], imb_rows[:], ident_b[:])
+        nc.vector.tensor_copy(out=imb_col[:], in_=imb_ps[:, 0:NT])
+        wfull = scr.tile([P, 4, UG, D], F32, name="wfull", tag="scr")
+        nc.vector.tensor_copy(out=wfull[:], in_=lnw[:, :, 0:D].unsqueeze(2).to_broadcast([P, 4, UG, D]))
+        wflat = wfull[:].rearrange("q k g d -> q k (g d)")
+        for i3 in range(UT):
+            wps = psum.tile([P, 4, P], F32, name="wps", tag="a4")
+            for k in range(4):
+                nc.tensor.transpose(wps[:, k, :], wflat[:, k, i3 * P:(i3 + 1) * P], ident_f[:])
+            nc.vector.tensor_copy(out=wcol[:, i3, :], in_=wps[:, :, 0])
+
+        PIECE = 1024
+        for c0 in range(0, K, PIECE):
+            cs = slice(c0, c0 + PIECE)
+            for bt in range(2):
+                nc.scalar.activation(out=pol[:, 2 + bt, cs], in_=pol[:, bt, cs], func=ACT.Sin)
+                if c0 == 0 and bt == 0:
+                    nc.scalar.activation(out=pol[:, bt, cs], in_=pol[:, bt, cs], func=ACT.Abs, bias=tstz[:])
+                else:
+                    nc.scalar.activation(out=pol[:, bt, cs], in_=pol[:, bt, cs], func=ACT.Abs)
+                nc.scalar.activation(out=pol[:, bt, cs], in_=pol[:, bt, cs], func=ACT.Sin, scale=-1.0,
+                                     bias=math.pi / 2.0)
+                lamf = lams[bt][:].rearrange("q g d -> q (g d)")
+                nc.vector.tensor_tensor(out=pol[:, bt, cs], in0=pol[:, bt, cs], in1=lamf[:, cs], op=ALU.mult)
+                nc.vector.tensor_tensor(out=pol[:, 2 + bt, cs], in0=pol[:, 2 + bt, cs], in1=lamf[:, cs], op=ALU.mult)
+
+        for j in range(CHUNKS):
+            nxt = prep(j + 1, None) if j + 1 < CHUNKS else None
+            for i in range(j * (NC // P), (j + 1) * (NC // P)):
+                linear_tile(i, codes[0], codes[1])
+                if i % UT == UT - 1:
+                    finish(i // UT)
+            codes = nxt

@@ -28,8 +28,8 @@ NT = K // P
 UT = 3
 UG = UT * P // D
 TWO_PI = 2.0 * math.pi
-SB_UNITS = {(j, 3) for j in range(1, 6)}
-Y4_ON_VECTOR = ()
+SB_UNITS = ()
+Y4_ON_VECTOR = range(24)
 
 FLOPS = 2 * (2 * B) * K * K + 2 * 2 * B * D * F * F
 

@@ -29,6 +29,9 @@ UT = 3
 UG = UT * P // D
 TWO_PI = 2.0 * math.pi
 SB_UNITS = ()
+AV_UNITS = ()
+GB_UNITS = {(j, g) for j in range(6) for g in (1, 2, 4, 5)}
+RELU_ON_VECTOR = ()
 Y4_ON_VECTOR = range(24)
 
 FLOPS = 2 * (2 * B) * K * K + 2 * 2 * B * D * F * F
@@ -110,7 +113,7 @@ def tile_eulerinteractionlayer_pa_kernel(
                 nc.sync.dma_start(out=xraw[:], in_=xsrc[m])
             words = xraw[:].bitcast(F32)
             for h in range(PASSES // 2):
-                xt = psum.tile([P, 2, 2, P], F32, name="xt", tag="tT")
+                xt = psum.tile([P, 2, 2, P], F32, name="xt", tag="acc", bufs=4)
                 for gi in range(2):
                     g = 2 * h + gi
                     for u in range(2):
@@ -135,10 +138,19 @@ def tile_eulerinteractionlayer_pa_kernel(
                 wraw = raws[g] if raws else load_w(j, g)
                 planes = plp.tile([P, 4, NC], BF16, name="planes", tag="planes")
                 for t in range(4):
-                    nc.scalar.activation(out=planes[:, t, :], in_=wraw[:, t, :].bitcast(FP8), func=ACT.Copy,
-                                         scale=wsc[:, g, t:t + 1])
+                    if (j, g) in AV_UNITS:
+                        nc.vector.tensor_scalar(out=planes[:, t, :], in0=wraw[:, t, :].bitcast(FP8),
+                                                scalar1=wsc[:, g, t:t + 1], scalar2=None, op0=ALU.mult)
+                    else:
+                        nc.scalar.activation(out=planes[:, t, :], in_=wraw[:, t, :].bitcast(FP8), func=ACT.Copy,
+                                             scale=wsc[:, g, t:t + 1])
                 grp = grp_pool.tile([P, NC, 4], BF16, name="grp", tag="grp", align_bytes=64)
-                if (j, g) in SB_UNITS:
+                if (j, g) in GB_UNITS:
+                    for c0 in range(0, NC, NC // 2):
+                        nc.gpsimd.tensor_scalar(out=grp[:, c0:c0 + NC // 2, :],
+                                                in0=planes[:, :, c0:c0 + NC // 2].rearrange("q t n -> q n t"),
+                                                scalar1=1.0, scalar2=0.0, op0=ALU.mult, op1=ALU.add)
+                elif (j, g) in SB_UNITS:
                     nc.scalar.copy(out=grp[:], in_=planes[:].rearrange("q t n -> q n t"))
                 else:
                     nc.vector.tensor_copy(out=grp[:], in_=planes[:].rearrange("q t n -> q n t"))
@@ -149,7 +161,7 @@ def tile_eulerinteractionlayer_pa_kernel(
         def linear_tile(i, wc, ws):
             li = i % (NC // P)
             cols = slice(li * P, (li + 1) * P)
-            acc = psum.tile([P, MT * P], F32, name="acc", tag="acc")
+            acc = psum.tile([P, MT * P], F32, name="acc", tag="acc", bufs=4)
             for g in range(PASSES):
                 nc.tensor.matmul_mx(
                     out=acc[:],
@@ -157,9 +169,16 @@ def tile_eulerinteractionlayer_pa_kernel(
                     rhs=xc[:, g, :].bitcast(FP8X4), rhs_scale=xs[:, g, :],
                     start=(g == 0), stop=(g == PASSES - 1),
                 )
+            return acc
+
+        def back_tile(i, acc):
             a_t = atp.tile([P, MT * P], F32, name="a_t", tag="a_t")
-            nc.scalar.activation(out=a_t[:], in_=acc[:], func=ACT.Relu, bias=imb_col[:, i:i + 1])
-            a4 = psum.tile([P, MT, P], F32, name="a4", tag="a4")
+            if i in RELU_ON_VECTOR:
+                nc.vector.tensor_scalar(out=a_t[:], in0=acc[:], scalar1=imb_col[:, i:i + 1], scalar2=0.0,
+                                        op0=ALU.add, op1=ALU.max)
+            else:
+                nc.scalar.activation(out=a_t[:], in_=acc[:], func=ACT.Relu, bias=imb_col[:, i:i + 1])
+            a4 = psum.tile([P, MT, P], F32, name="a4", tag="a4", bufs=2)
             for m in range(MT):
                 nc.tensor.transpose(a4[:, m, :], a_t[:, m * P:(m + 1) * P], ident_f[:])
             ncols = slice(i * P, (i + 1) * P)
@@ -185,7 +204,7 @@ def tile_eulerinteractionlayer_pa_kernel(
 
         def affine_tile(i):
             ncols = slice(i * P, (i + 1) * P)
-            t_t = psum.tile([P, MT * P], F32, name="t_t", tag="tT")
+            t_t = psum.tile([P, MT * P], F32, name="t_t", tag="tT", bufs=1)
             for m in range(MT):
                 nc.tensor.transpose(t_t[:, m * P:(m + 1) * P], pol[:, m, ncols], ident_f[:])
             y_t = atp.tile([P, MT * P], F32, name="y_t", tag="y_t")
@@ -194,7 +213,7 @@ def tile_eulerinteractionlayer_pa_kernel(
                 nc.scalar.activation(out=y_t[:, half], in_=t_t[:, half], func=ACT.Identity,
                                      scale=wcol[:, i % UT, 2 * rp:2 * rp + 1],
                                      bias=wcol[:, i % UT, 2 * rp + 1:2 * rp + 2])
-            y4 = psum.tile([P, MT, P], F32, name="y4", tag="y4")
+            y4 = psum.tile([P, MT, P], F32, name="y4", tag="y4", bufs=1)
             for m in range(MT):
                 nc.tensor.transpose(y4[:, m, :], y_t[:, m * P:(m + 1) * P], ident_f[:])
             if i in Y4_ON_VECTOR:
@@ -228,7 +247,7 @@ def tile_eulerinteractionlayer_pa_kernel(
                 lw = lraw[:].bitcast(F32)
                 lt = ltp.tile([P, D // 2, P], F32, name="lt", tag="lt")
                 for q in range(3):
-                    tpb = psum.tile([P, 4, P], F32, name="tpb", tag="tT")
+                    tpb = psum.tile([P, 4, P], F32, name="tpb", tag="acc", bufs=4)
                     for i in range(4):
                         nc.tensor.transpose(tpb[:, i, :], lw[:, 4 * q + i:K // 2:D // 2], ident_f[:])
                     nc.vector.tensor_copy(out=lt[:, 4 * q:4 * q + 4, :], in_=tpb[:])
@@ -237,7 +256,7 @@ def tile_eulerinteractionlayer_pa_kernel(
                     lam = scr.tile([P, F, D], F32, name="lam", tag="scr")
                     lams.append(lam)
                 for dq in range(D // 4):
-                    pp = psum.tile([P, 4, P], F32, name="pp", tag="y4")
+                    pp = psum.tile([P, 4, P], F32, name="pp", tag="a4", bufs=2)
                     for i in range(4):
                         d = 4 * dq + i
                         nc.tensor.matmul(out=pp[:, i, :], lhsT=ltb[:, d // 2, :, d % 2], rhs=io_sb[:],
@@ -254,14 +273,14 @@ def tile_eulerinteractionlayer_pa_kernel(
                                                        in0=kt[:].rearrange("q i g -> q g i"), scalar=-TWO_PI,
                                                        in1=ppv, op0=ALU.mult, op1=ALU.add)
 
-        imb_ps = psum.tile([P, P], BF16, name="imb_ps", tag="a4")
+        imb_ps = psum.tile([P, P], BF16, name="imb_ps", tag="tT", bufs=1)
         nc.tensor.transpose(imb_ps[:], imb_rows[:], ident_b[:])
         nc.vector.tensor_copy(out=imb_col[:], in_=imb_ps[:, 0:NT])
         wfull = scr.tile([P, 4, UG, D], F32, name="wfull", tag="scr")
         nc.vector.tensor_copy(out=wfull[:], in_=lnw[:, :, 0:D].unsqueeze(2).to_broadcast([P, 4, UG, D]))
         wflat = wfull[:].rearrange("q k g d -> q k (g d)")
         for i3 in range(UT):
-            wps = psum.tile([P, 4, P], F32, name="wps", tag="a4")
+            wps = psum.tile([P, 4, P], F32, name="wps", tag="y4", bufs=1)
             for k in range(4):
                 nc.tensor.transpose(wps[:, k, :], wflat[:, k, i3 * P:(i3 + 1) * P], ident_f[:])
             nc.vector.tensor_copy(out=wcol[:, i3, :], in_=wps[:, :, 0])
@@ -283,8 +302,10 @@ def tile_eulerinteractionlayer_pa_kernel(
 
         for j in range(CHUNKS):
             nxt = prep(j + 1, None) if j + 1 < CHUNKS else None
-            for i in range(j * (NC // P), (j + 1) * (NC // P)):
-                linear_tile(i, codes[0], codes[1])
+            tiles = range(j * (NC // P), (j + 1) * (NC // P))
+            accs = [linear_tile(i, codes[0], codes[1]) for i in tiles]
+            for i in tiles:
+                back_tile(i, accs[i % (NC // P)])
                 if i % UT == UT - 1:
                     finish(i // UT)
             codes = nxt

@@ -30,9 +30,10 @@ UG = UT * P // D
 TWO_PI = 2.0 * math.pi
 SB_UNITS = ()
 AV_UNITS = ()
-GB_UNITS = {(j, g) for j in range(6) for g in (1, 2, 4, 5)}
+GB_UNITS = ()
 RELU_ON_VECTOR = ()
-Y4_ON_VECTOR = range(24)
+FAST_IL = True
+Y4_ON_VECTOR = (0, 3, 6, 9, 12, 15, 18, 21, 22, 23)
 
 FLOPS = 2 * (2 * B) * K * K + 2 * 2 * B * D * F * F
 
@@ -96,15 +97,17 @@ def tile_eulerinteractionlayer_pa_kernel(
         pol = const.tile([P, MT, K], F32, name="pol")
         polv = pol[:].rearrange("q m (g d) -> q m g d", d=D)
 
-        tst = const.tile([P, 1], F32, name="tst")
-        nc.vector.memset(tst[:], 0.75)
-        tsti = const.tile([P, 1], I32, name="tsti")
-        nc.vector.tensor_copy(out=tsti[:], in_=tst[:])
-        tstf = const.tile([P, 1], F32, name="tstf")
-        nc.vector.tensor_copy(out=tstf[:], in_=tsti[:])
-        tstz = const.tile([P, 1], F32, name="tstz")
-        nc.vector.tensor_scalar(out=tstz[:], in0=tstf[:], scalar1=-1.0, scalar2=None, op0=ALU.add)
 
+        def quantise_x(m, h, xg):
+            for gi in range(2):
+                g = 2 * h + gi
+                nc.vector.quantize_mx(
+                    out=xc[:, g, m * P:(m + 1) * P].bitcast(FP8X4),
+                    scales=xs[:, g, m * P:(m + 1) * P],
+                    in_=xg[:, gi, :, :].rearrange("q r t -> q (r t)"),
+                )
+
+        held = None
         for m in range(MT):
             if m < 3:
                 xraw = xraws[m]
@@ -123,17 +126,15 @@ def tile_eulerinteractionlayer_pa_kernel(
                     out=xg[:].rearrange("q a r t -> q (a r t)").bitcast(F32).rearrange("q (a r u) -> q a r u", a=2, u=2),
                     in_=xt[:].rearrange("q a u r -> q a r u"),
                 )
-                for gi in range(2):
-                    g = 2 * h + gi
-                    nc.vector.quantize_mx(
-                        out=xc[:, g, m * P:(m + 1) * P].bitcast(FP8X4),
-                        scales=xs[:, g, m * P:(m + 1) * P],
-                        in_=xg[:, gi, :, :].rearrange("q r t -> q (r t)"),
-                    )
+                if held:
+                    quantise_x(held[0], held[1], held[2])
+                held = (m, h, xg)
+        quantise_x(held[0], held[1], held[2])
 
         def prep(j, raws):
             wc = wcp.tile([P, PASSES, NC], U32, name="wc", tag="wc", align_bytes=64)
             ws = wcp.tile([P, PASSES, NC], U8, name="ws", tag="ws", align_bytes=64)
+            pending = []
             for g in range(PASSES):
                 wraw = raws[g] if raws else load_w(j, g)
                 planes = plp.tile([P, 4, NC], BF16, name="planes", tag="planes")
@@ -152,10 +153,17 @@ def tile_eulerinteractionlayer_pa_kernel(
                                                 scalar1=1.0, scalar2=0.0, op0=ALU.mult, op1=ALU.add)
                 elif (j, g) in SB_UNITS:
                     nc.scalar.copy(out=grp[:], in_=planes[:].rearrange("q t n -> q n t"))
+                elif FAST_IL:
+                    nc.vector.tensor_copy(out=grp[:].rearrange("q (c i) t -> q c t i", i=4),
+                                          in_=planes[:].rearrange("q t (c i) -> q c t i", i=4))
                 else:
                     nc.vector.tensor_copy(out=grp[:], in_=planes[:].rearrange("q t n -> q n t"))
-                nc.vector.quantize_mx(out=wc[:, g, :].bitcast(FP8X4), scales=ws[:, g, :],
-                                      in_=grp[:].rearrange("q n t -> q (n t)"))
+                pending.append((g, grp))
+                if g == PASSES - 1 or len(pending) == 2:
+                    for gq, gt in (pending if g == PASSES - 1 else pending[0:1]):
+                        nc.vector.quantize_mx(out=wc[:, gq, :].bitcast(FP8X4), scales=ws[:, gq, :],
+                                              in_=gt[:].rearrange("q n t -> q (n t)"))
+                    pending = pending[1:]
             return wc, ws
 
         def linear_tile(i, wc, ws):
@@ -223,11 +231,17 @@ def tile_eulerinteractionlayer_pa_kernel(
 
         def finish(u):
             normalise(u)
+            last_unit = u == NT // UT - 1
             for i in range(UT * u, UT * (u + 1)):
                 affine_tile(i)
+                if last_unit:
+                    for rp in range(2):
+                        nc.sync.dma_start(out=outv[rp][:, :, i * P:(i + 1) * P],
+                                          in_=pol[:, 2 * rp:2 * rp + 2, i * P:(i + 1) * P])
             ucols = slice(u * UT * P, (u + 1) * UT * P)
-            for rp in range(2):
-                nc.sync.dma_start(out=outv[rp][:, :, ucols], in_=pol[:, 2 * rp:2 * rp + 2, ucols])
+            if not last_unit:
+                for rp in range(2):
+                    nc.sync.dma_start(out=outv[rp][:, :, ucols], in_=pol[:, 2 * rp:2 * rp + 2, ucols])
 
         codes = prep(0, first_w)
 
@@ -255,6 +269,7 @@ def tile_eulerinteractionlayer_pa_kernel(
                 if x == 0:
                     lam = scr.tile([P, F, D], F32, name="lam", tag="scr")
                     lams.append(lam)
+                waiting = []
                 for dq in range(D // 4):
                     pp = psum.tile([P, 4, P], F32, name="pp", tag="a4", bufs=2)
                     for i in range(4):
@@ -269,9 +284,14 @@ def tile_eulerinteractionlayer_pa_kernel(
                     else:
                         kt = ktp.tile([P, 4, P], I32, name="kt", tag="kt")
                         nc.vector.tensor_scalar(out=kt[:], in0=pp[:], scalar1=1.0 / TWO_PI, scalar2=None, op0=ALU.mult)
-                        nc.vector.scalar_tensor_tensor(out=polv[:, bt, :, 4 * dq:4 * dq + 4],
-                                                       in0=kt[:].rearrange("q i g -> q g i"), scalar=-TWO_PI,
-                                                       in1=ppv, op0=ALU.mult, op1=ALU.add)
+                        waiting.append((dq, kt, ppv))
+                        last = dq == D // 4 - 1
+                        if last or len(waiting) == 2:
+                            for dw, kw, pw in (waiting if last else waiting[0:1]):
+                                nc.vector.scalar_tensor_tensor(out=polv[:, bt, :, 4 * dw:4 * dw + 4],
+                                                               in0=kw[:].rearrange("q i g -> q g i"), scalar=-TWO_PI,
+                                                               in1=pw, op0=ALU.mult, op1=ALU.add)
+                            waiting = waiting[1:]
 
         imb_ps = psum.tile([P, P], BF16, name="imb_ps", tag="tT", bufs=1)
         nc.tensor.transpose(imb_ps[:], imb_rows[:], ident_b[:])
@@ -290,10 +310,7 @@ def tile_eulerinteractionlayer_pa_kernel(
             cs = slice(c0, c0 + PIECE)
             for bt in range(2):
                 nc.scalar.activation(out=pol[:, 2 + bt, cs], in_=pol[:, bt, cs], func=ACT.Sin)
-                if c0 == 0 and bt == 0:
-                    nc.scalar.activation(out=pol[:, bt, cs], in_=pol[:, bt, cs], func=ACT.Abs, bias=tstz[:])
-                else:
-                    nc.scalar.activation(out=pol[:, bt, cs], in_=pol[:, bt, cs], func=ACT.Abs)
+                nc.scalar.activation(out=pol[:, bt, cs], in_=pol[:, bt, cs], func=ACT.Abs)
                 nc.scalar.activation(out=pol[:, bt, cs], in_=pol[:, bt, cs], func=ACT.Sin, scale=-1.0,
                                      bias=math.pi / 2.0)
                 lamf = lams[bt][:].rearrange("q g d -> q (g d)")

@@ -33,7 +33,8 @@ AV_UNITS = ()
 GB_UNITS = ()
 RELU_ON_VECTOR = ()
 FAST_IL = True
-Y4_ON_VECTOR = (0, 3, 6, 9, 12, 15, 18, 21, 22, 23)
+Y4_ON_VECTOR = (22, 23)
+V_WIDENS = (0, 2, 4)
 
 FLOPS = 2 * (2 * B) * K * K + 2 * 2 * B * D * F * F
 
@@ -139,7 +140,7 @@ def tile_eulerinteractionlayer_pa_kernel(
                 wraw = raws[g] if raws else load_w(j, g)
                 planes = plp.tile([P, 4, NC], BF16, name="planes", tag="planes")
                 for t in range(4):
-                    if (j, g) in AV_UNITS:
+                    if t == 3 and g in V_WIDENS:
                         nc.vector.tensor_scalar(out=planes[:, t, :], in0=wraw[:, t, :].bitcast(FP8),
                                                 scalar1=wsc[:, g, t:t + 1], scalar2=None, op0=ALU.mult)
                     else:
@@ -192,23 +193,34 @@ def tile_eulerinteractionlayer_pa_kernel(
             ncols = slice(i * P, (i + 1) * P)
             nc.vector.tensor_tensor(out=pol[:, :, ncols], in0=a4[:], in1=pol[:, :, ncols], op=ALU.add)
 
-        def normalise(u):
+        def normalise(u, parts):
             g0 = u * UG
-            o = polv[:, :, g0:g0 + UG, :]
-            s1 = stp.tile([P, MT, UG], F32, name="s1", tag="s1")
-            nc.vector.tensor_reduce(out=s1[:], in_=o, axis=AX.X, op=ALU.add)
-            nc.vector.scalar_tensor_tensor(out=o, in0=s1[:].unsqueeze(3).to_broadcast([P, MT, UG, D]),
-                                           scalar=-1.0 / D, in1=o, op0=ALU.mult, op1=ALU.add)
-            sq = scr.tile([P, MT, UG, D], F32, name="sq", tag="scr")
-            nc.scalar.activation(out=sq[:], in_=o, func=ACT.Square)
-            s2 = stp.tile([P, MT, UG], F32, name="s2", tag="s2")
-            nc.vector.tensor_reduce(out=s2[:], in_=sq[:], axis=AX.X, op=ALU.add)
-            sd = stp.tile([P, MT, UG], F32, name="sd", tag="sd")
-            nc.scalar.activation(out=sd[:], in_=s2[:], func=ACT.Sqrt, scale=1.0 / D, bias=LN_EPS)
-            rho = stp.tile([P, MT, UG], F32, name="rho", tag="rho")
-            nc.vector.reciprocal(out=rho[:], in_=sd[:])
-            nc.vector.tensor_tensor(out=o, in0=o, in1=rho[:].unsqueeze(3).to_broadcast([P, MT, UG, D]),
-                                    op=ALU.mult)
+            data = [polv[:, m0:m1, g0:g0 + UG, :] for m0, m1 in parts]
+            shapes = [[P, m1 - m0, UG] for m0, m1 in parts]
+            sums = []
+            for o, shape in zip(data, shapes):
+                s1 = stp.tile(shape, F32, name="s1", tag="s1")
+                nc.vector.tensor_reduce(out=s1[:], in_=o, axis=AX.X, op=ALU.add)
+                sums.append(s1)
+            for o, shape, s1 in zip(data, shapes, sums):
+                nc.vector.scalar_tensor_tensor(out=o, in0=s1[:].unsqueeze(3).to_broadcast(shape + [D]),
+                                               scalar=-1.0 / D, in1=o, op0=ALU.mult, op1=ALU.add)
+            squares = []
+            for o, shape in zip(data, shapes):
+                sq = scr.tile(shape + [D], F32, name="sq", tag="scr")
+                nc.scalar.activation(out=sq[:], in_=o, func=ACT.Square)
+                squares.append(sq)
+            factors = []
+            for sq, shape in zip(squares, shapes):
+                s2 = stp.tile(shape, F32, name="s2", tag="s2")
+                nc.vector.tensor_reduce(out=s2[:], in_=sq[:], axis=AX.X, op=ALU.add)
+                sd = stp.tile(shape, F32, name="sd", tag="sd")
+                nc.scalar.activation(out=sd[:], in_=s2[:], func=ACT.Sqrt, scale=1.0 / D, bias=LN_EPS)
+                rho = stp.tile(shape, F32, name="rho", tag="rho")
+                nc.vector.reciprocal(out=rho[:], in_=sd[:])
+                factors.append(rho)
+            for o, shape, rho in zip(data, shapes, factors):
+                nc.vector.tensor_tensor(out=o, in0=o, in1=rho[:].unsqueeze(3).to_broadcast(shape + [D]), op=ALU.mult)
 
         def affine_tile(i):
             ncols = slice(i * P, (i + 1) * P)
@@ -230,8 +242,8 @@ def tile_eulerinteractionlayer_pa_kernel(
                 nc.scalar.copy(out=pol[:, :, ncols], in_=y4[:])
 
         def finish(u):
-            normalise(u)
             last_unit = u == NT // UT - 1
+            normalise(u, [(0, 2), (2, MT)] if last_unit else [(0, MT)])
             for i in range(UT * u, UT * (u + 1)):
                 affine_tile(i)
                 if last_unit:
@@ -264,7 +276,7 @@ def tile_eulerinteractionlayer_pa_kernel(
                     tpb = psum.tile([P, 4, P], F32, name="tpb", tag="acc", bufs=4)
                     for i in range(4):
                         nc.tensor.transpose(tpb[:, i, :], lw[:, 4 * q + i:K // 2:D // 2], ident_f[:])
-                    nc.vector.tensor_copy(out=lt[:, 4 * q:4 * q + 4, :], in_=tpb[:])
+                    nc.scalar.copy(out=lt[:, 4 * q:4 * q + 4, :], in_=tpb[:])
                 ltb = lt[:].rearrange("q a b -> q (a b)").bitcast(BF16).rearrange("q (a b e) -> q a b e", a=D // 2, e=2)
                 if x == 0:
                     lam = scr.tile([P, F, D], F32, name="lam", tag="scr")

@@ -155,8 +155,8 @@ def tile_eulerinteractionlayer_pa_kernel(
                 elif (j, g) in SB_UNITS:
                     nc.scalar.copy(out=grp[:], in_=planes[:].rearrange("q t n -> q n t"))
                 elif FAST_IL:
-                    nc.vector.tensor_copy(out=grp[:].rearrange("q (c i) t -> q c t i", i=4),
-                                          in_=planes[:].rearrange("q t (c i) -> q c t i", i=4))
+                    nc.vector.tensor_copy(out=grp[:].rearrange("q (c i) t -> q c t i", i=8),
+                                          in_=planes[:].rearrange("q t (c i) -> q c t i", i=8))
                 else:
                     nc.vector.tensor_copy(out=grp[:], in_=planes[:].rearrange("q t n -> q n t"))
                 pending.append((g, grp))

@@ -214,10 +214,8 @@ def tile_eulerinteractionlayer_pa_kernel(
             for sq, shape in zip(squares, shapes):
                 s2 = stp.tile(shape, F32, name="s2", tag="s2")
                 nc.vector.tensor_reduce(out=s2[:], in_=sq[:], axis=AX.X, op=ALU.add)
-                sd = stp.tile(shape, F32, name="sd", tag="sd")
-                nc.scalar.activation(out=sd[:], in_=s2[:], func=ACT.Sqrt, scale=1.0 / D, bias=LN_EPS)
                 rho = stp.tile(shape, F32, name="rho", tag="rho")
-                nc.vector.reciprocal(out=rho[:], in_=sd[:])
+                nc.scalar.activation(out=rho[:], in_=s2[:], func=ACT.Abs_reciprocal_sqrt, scale=1.0 / D, bias=LN_EPS)
                 factors.append(rho)
             for o, shape, rho in zip(data, shapes, factors):
                 nc.vector.tensor_tensor(out=o, in0=o, in1=rho[:].unsqueeze(3).to_broadcast(shape + [D]), op=ALU.mult)

@@ -21,20 +21,16 @@ AX = mybir.AxisListType
 
 P = 128
 PASSES = K // 512
-NC = 512
-CHUNKS = K // NC
 MT = 4
-NT = K // P
-UT = 3
-UG = UT * P // D
+ROWS = MT * P
+UNITS = 4
+GU = F // UNITS
+UC = GU * D
+DL = P // GU
+DQ = D // DL
+TG = 3
 TWO_PI = 2.0 * math.pi
-SB_UNITS = ()
-AV_UNITS = ()
-GB_UNITS = ()
-RELU_ON_VECTOR = ()
-FAST_IL = True
-Y4_ON_VECTOR = (22, 23)
-V_WIDENS = (0, 2, 4)
+V_WIDENS = (0, 2, 4, 5)
 
 FLOPS = 2 * (2 * B) * K * K + 2 * 2 * B * D * F * F
 
@@ -46,18 +42,17 @@ def tile_eulerinteractionlayer_pa_kernel(
     nc = tc.nc
     with ExitStack() as ctx:
         const = ctx.enter_context(tc.tile_pool(name="const", bufs=1))
-        rawp = ctx.enter_context(tc.tile_pool(name="rawp", bufs=3))
-        xgp = ctx.enter_context(tc.tile_pool(name="xgp", bufs=2))
-        ltp = ctx.enter_context(tc.tile_pool(name="ltp", bufs=2))
-        ktp = ctx.enter_context(tc.tile_pool(name="ktp", bufs=2))
-        wrawp = ctx.enter_context(tc.tile_pool(name="wrawp", bufs=8))
+        wrawp = ctx.enter_context(tc.tile_pool(name="wrawp", bufs=6))
         plp = ctx.enter_context(tc.tile_pool(name="plp", bufs=3))
         grp_pool = ctx.enter_context(tc.tile_pool(name="grpp", bufs=3))
         wcp = ctx.enter_context(tc.tile_pool(name="wcp", bufs=2))
-        scr = ctx.enter_context(tc.tile_pool(name="scr", bufs=3))
-        atp = ctx.enter_context(tc.tile_pool(name="atp", bufs=3))
-        stp = ctx.enter_context(tc.tile_pool(name="stp", bufs=2))
         psum = ctx.enter_context(tc.psum_pool(name="psum", bufs=2))
+
+        def bank(shape, dtype, name):
+            return psum.tile(shape, dtype, name=name, tag="ring", bufs=6)
+
+        def stat_bank(name):
+            return psum.tile([P, ROWS], F32, name=name, tag="stat", bufs=2)
 
         wview = im_w_bytes.rearrange("(g q t) n -> g q t n", q=P, t=4)
         outv = [o.rearrange("(t q) g d -> q t (g d)", q=P) for o in (out_0, out_1)]
@@ -65,112 +60,204 @@ def tile_eulerinteractionlayer_pa_kernel(
         p2 = p.rearrange("b f d -> b (f d)")
         xsrc = [r2[0:P, :], r2[P:2 * P, :], p2[0:P, :], p2[P:2 * P, :]]
 
-        def load_w(j, g):
-            wraw = wrawp.tile([P, 4, NC], U8, name="wraw", tag="wraw")
-            nc.sync.dma_start(out=wraw[:], in_=wview[g][:, :, j * NC:(j + 1) * NC])
+        def load_w(u, g):
+            wraw = wrawp.tile([P, 4, UC], U8, name="wraw", tag="wraw")
+            nc.sync.dma_start(out=wraw[:], in_=wview[g][:, :, u * UC:(u + 1) * UC])
             return wraw
 
         wsc = const.tile([P, PASSES, 4], F32, name="wsc")
-        nc.sync.dma_start(out=wsc[:], in_=im_w_scale.rearrange("(g q t) o -> q g (t o)", q=P, t=4))
-        first_w = []
-        xraws = []
-        for g in range(PASSES):
-            first_w.append(load_w(0, g))
-            if g < 3:
-                xraw = rawp.tile([P, K], BF16, name="xraw", tag="raw")
-                nc.sync.dma_start(out=xraw[:], in_=xsrc[g])
-                xraws.append(xraw)
-
         ident_f = const.tile([P, P], F32, name="ident_f")
-        make_identity(nc, ident_f[:])
         ident_b = const.tile([P, P], BF16, name="ident_b")
-        make_identity(nc, ident_b[:])
         io_sb = const.tile([P, P], BF16, name="io_sb")
         bias_sb = const.tile([P, 2, P], BF16, name="bias_sb")
-        nc.vector.memset(bias_sb[:], 0.0)
         imb_rows = const.tile([P, P], BF16, name="imb_rows")
-        nc.vector.memset(imb_rows[:], 0.0)
-        imb_col = const.tile([P, NT], F32, name="imb_col")
+        imb_col = const.tile([P, UNITS * DQ], F32, name="imb_col")
         lnw = const.tile([P, 4, 32], BF16, name="lnw")
-        wcol = const.tile([P, UT, 4], F32, name="wcol")
-        xc = const.tile([P, PASSES, MT * P], U32, name="xc", align_bytes=64)
-        xs = const.tile([P, PASSES, MT * P], U8, name="xs", align_bytes=64)
+        lmask = const.tile([P, DL], F32, name="lmask")
+        lnsel = const.tile([P, 4, DQ, DL], F32, name="lnsel")
+        lncol = const.tile([P, 4, DQ], F32, name="lncol")
+        negw = const.tile([P, 2, DQ], F32, name="negw")
+        xc = const.tile([P, PASSES, ROWS], U32, name="xc", align_bytes=64)
+        xs = const.tile([P, PASSES, ROWS], U8, name="xs", align_bytes=64)
         pol = const.tile([P, MT, K], F32, name="pol")
-        polv = pol[:].rearrange("q m (g d) -> q m g d", d=D)
+        polp = pol[:].rearrange("q m (u a g l) -> q m u a g l", u=UNITS, a=DQ, g=GU, l=DL)
 
+        def quantise_w(wc, ws, g, grp):
+            flat = grp[:].rearrange("q c t -> q (c t)")
+            for c0, c1 in ((0, 512), (512, UC)):
+                nc.vector.quantize_mx(out=wc[:, g, c0:c1].bitcast(FP8X4), scales=ws[:, g, c0:c1],
+                                      in_=flat[:, 4 * c0:4 * c1])
 
-        def quantise_x(m, h, xg):
-            for gi in range(2):
-                g = 2 * h + gi
-                nc.vector.quantize_mx(
-                    out=xc[:, g, m * P:(m + 1) * P].bitcast(FP8X4),
-                    scales=xs[:, g, m * P:(m + 1) * P],
-                    in_=xg[:, gi, :, :].rearrange("q r t -> q (r t)"),
-                )
+        def prep_start():
+            wc = wcp.tile([P, PASSES, UC], U32, name="wc", tag="wc", align_bytes=64)
+            ws = wcp.tile([P, PASSES, UC], U8, name="ws", tag="ws", align_bytes=64)
+            return [wc, ws, None]
 
-        held = None
-        for m in range(MT):
-            if m < 3:
-                xraw = xraws[m]
-            else:
-                xraw = rawp.tile([P, K], BF16, name="xraw", tag="raw")
-                nc.sync.dma_start(out=xraw[:], in_=xsrc[m])
-            words = xraw[:].bitcast(F32)
-            for h in range(PASSES // 2):
-                xt = psum.tile([P, 2, 2, P], F32, name="xt", tag="acc", bufs=4)
+        def prep_pass(state, g, wraw):
+            wc, ws, waiting = state
+            planes = plp.tile([P, 4, UC], BF16, name="planes", tag="planes")
+            for t in range(4):
+                if t == 3 and g in V_WIDENS:
+                    nc.vector.tensor_scalar(out=planes[:, t, :], in0=wraw[:, t, :].bitcast(FP8),
+                                            scalar1=wsc[:, g, t:t + 1], scalar2=None, op0=ALU.mult)
+                else:
+                    nc.scalar.activation(out=planes[:, t, :], in_=wraw[:, t, :].bitcast(FP8), func=ACT.Copy,
+                                         scale=wsc[:, g, t:t + 1])
+            grp = grp_pool.tile([P, UC, 4], BF16, name="grp", tag="grp", align_bytes=64)
+            nc.vector.tensor_copy(out=grp[:].rearrange("q (a g l) t -> q g a l t", a=DQ, g=GU, l=DL),
+                                  in_=planes[:].rearrange("q t (g a l) -> q g a l t", g=GU, a=DQ, l=DL))
+            if waiting:
+                quantise_w(wc, ws, g - 1, waiting)
+            if g == PASSES - 1:
+                quantise_w(wc, ws, g, grp)
+            state[2] = grp
+
+        with ExitStack() as head:
+            rawp = head.enter_context(tc.tile_pool(name="rawp", bufs=3))
+            xgp = head.enter_context(tc.tile_pool(name="xgp", bufs=2))
+            ltp = head.enter_context(tc.tile_pool(name="ltp", bufs=2))
+            ktp = head.enter_context(tc.tile_pool(name="ktp", bufs=2))
+            lamp = head.enter_context(tc.tile_pool(name="lamp", bufs=2))
+
+            nc.sync.dma_start(out=wsc[:], in_=im_w_scale.rearrange("(g q t) o -> q g (t o)", q=P, t=4))
+            first_w = []
+            xraws = []
+            for g in range(PASSES):
+                first_w.append(load_w(0, g))
+                if g < 3:
+                    xraw = rawp.tile([P, K], BF16, name="xraw", tag="raw")
+                    nc.sync.dma_start(out=xraw[:], in_=xsrc[g])
+                    xraws.append(xraw)
+
+            make_identity(nc, ident_f[:])
+            make_identity(nc, ident_b[:])
+            nc.vector.memset(bias_sb[:], 0.0)
+            nc.vector.memset(imb_rows[:], 0.0)
+
+            def quantise_x(m, h, xg):
                 for gi in range(2):
                     g = 2 * h + gi
-                    for u in range(2):
-                        nc.tensor.transpose(xt[:, gi, u, :], words[:, 256 * g + u:256 * (g + 1):2], ident_f[:])
-                xg = xgp.tile([P, 2, P, 4], BF16, name="xg", tag="xg", align_bytes=64)
-                nc.vector.tensor_copy(
-                    out=xg[:].rearrange("q a r t -> q (a r t)").bitcast(F32).rearrange("q (a r u) -> q a r u", a=2, u=2),
-                    in_=xt[:].rearrange("q a u r -> q a r u"),
-                )
-                if held:
-                    quantise_x(held[0], held[1], held[2])
-                held = (m, h, xg)
-        quantise_x(held[0], held[1], held[2])
+                    nc.vector.quantize_mx(
+                        out=xc[:, g, m * P:(m + 1) * P].bitcast(FP8X4),
+                        scales=xs[:, g, m * P:(m + 1) * P],
+                        in_=xg[:, gi, :, :].rearrange("q r t -> q (r t)"),
+                    )
 
-        def prep(j, raws):
-            wc = wcp.tile([P, PASSES, NC], U32, name="wc", tag="wc", align_bytes=64)
-            ws = wcp.tile([P, PASSES, NC], U8, name="ws", tag="ws", align_bytes=64)
-            pending = []
-            for g in range(PASSES):
-                wraw = raws[g] if raws else load_w(j, g)
-                planes = plp.tile([P, 4, NC], BF16, name="planes", tag="planes")
-                for t in range(4):
-                    if t == 3 and g in V_WIDENS:
-                        nc.vector.tensor_scalar(out=planes[:, t, :], in0=wraw[:, t, :].bitcast(FP8),
-                                                scalar1=wsc[:, g, t:t + 1], scalar2=None, op0=ALU.mult)
-                    else:
-                        nc.scalar.activation(out=planes[:, t, :], in_=wraw[:, t, :].bitcast(FP8), func=ACT.Copy,
-                                             scale=wsc[:, g, t:t + 1])
-                grp = grp_pool.tile([P, NC, 4], BF16, name="grp", tag="grp", align_bytes=64)
-                if (j, g) in GB_UNITS:
-                    for c0 in range(0, NC, NC // 2):
-                        nc.gpsimd.tensor_scalar(out=grp[:, c0:c0 + NC // 2, :],
-                                                in0=planes[:, :, c0:c0 + NC // 2].rearrange("q t n -> q n t"),
-                                                scalar1=1.0, scalar2=0.0, op0=ALU.mult, op1=ALU.add)
-                elif (j, g) in SB_UNITS:
-                    nc.scalar.copy(out=grp[:], in_=planes[:].rearrange("q t n -> q n t"))
-                elif FAST_IL:
-                    nc.vector.tensor_copy(out=grp[:].rearrange("q (c i) t -> q c t i", i=8),
-                                          in_=planes[:].rearrange("q t (c i) -> q c t i", i=8))
+            held = None
+            for m in range(MT):
+                if m < 3:
+                    xraw = xraws[m]
                 else:
-                    nc.vector.tensor_copy(out=grp[:], in_=planes[:].rearrange("q t n -> q n t"))
-                pending.append((g, grp))
-                if g == PASSES - 1 or len(pending) == 2:
-                    for gq, gt in (pending if g == PASSES - 1 else pending[0:1]):
-                        nc.vector.quantize_mx(out=wc[:, gq, :].bitcast(FP8X4), scales=ws[:, gq, :],
-                                              in_=gt[:].rearrange("q n t -> q (n t)"))
-                    pending = pending[1:]
-            return wc, ws
+                    xraw = rawp.tile([P, K], BF16, name="xraw", tag="raw")
+                    nc.sync.dma_start(out=xraw[:], in_=xsrc[m])
+                words = xraw[:].bitcast(F32)
+                for h in range(PASSES // 2):
+                    xt = bank([P, 2, 2, P], F32, "xt")
+                    for gi in range(2):
+                        g = 2 * h + gi
+                        for w in range(2):
+                            nc.tensor.transpose(xt[:, gi, w, :], words[:, 256 * g + w:256 * (g + 1):2], ident_f[:])
+                    xg = xgp.tile([P, 2, P, 4], BF16, name="xg", tag="xg", align_bytes=64)
+                    nc.vector.tensor_copy(
+                        out=xg[:].rearrange("q a r t -> q (a r t)").bitcast(F32).rearrange("q (a r w) -> q a r w", a=2, w=2),
+                        in_=xt[:].rearrange("q a w r -> q a r w"),
+                    )
+                    if held:
+                        quantise_x(held[0], held[1], held[2])
+                    held = (m, h, xg)
+            quantise_x(held[0], held[1], held[2])
 
-        def linear_tile(i, wc, ws):
-            li = i % (NC // P)
-            cols = slice(li * P, (li + 1) * P)
-            acc = psum.tile([P, MT * P], F32, name="acc", tag="acc", bufs=4)
+            codes = prep_start()
+            for g in range(PASSES):
+                prep_pass(codes, g, first_w[g])
+
+            nc.sync.dma_start(out=io_sb[:], in_=inter_orders)
+            nc.sync.dma_start(out=bias_sb[0:D, 0, :], in_=bias_lam.rearrange("o d g -> (o d) g"))
+            nc.sync.dma_start(out=bias_sb[0:D, 1, :], in_=bias_theta.rearrange("o d g -> (o d) g"))
+            imbv = im_b.rearrange("(u g a l) -> u a g l", u=UNITS, g=GU, a=DQ, l=DL)
+            for u in range(UNITS):
+                nc.sync.dma_start(out=imb_rows[u * DQ:(u + 1) * DQ, :].rearrange("a (g l) -> a g l", l=DL), in_=imbv[u])
+            for k, v in enumerate((norm_r_w, norm_r_b, norm_p_w, norm_p_b)):
+                nc.sync.dma_start(out=lnw[:, k, 0:D], in_=v.partition_broadcast(P))
+
+            lsrc = [log_lam.rearrange("b f d -> b (f d)"), theta.rearrange("b f d -> b (f d)")]
+            lams = []
+            for x in range(2):
+                for bt in range(2):
+                    lraw = rawp.tile([P, K], BF16, name="lraw", tag="raw")
+                    nc.sync.dma_start(out=lraw[:], in_=lsrc[x][bt * P:(bt + 1) * P, :])
+                    lw = lraw[:].bitcast(F32)
+                    lt = ltp.tile([P, D // 2, P], F32, name="lt", tag="lt")
+                    for q in range(3):
+                        tpb = bank([P, 4, P], F32, "tpb")
+                        for i in range(4):
+                            nc.tensor.transpose(tpb[:, i, :], lw[:, 4 * q + i:K // 2:D // 2], ident_f[:])
+                        nc.scalar.copy(out=lt[:, 4 * q:4 * q + 4, :], in_=tpb[:])
+                    ltb = lt[:].rearrange("q a b -> q (a b)").bitcast(BF16).rearrange("q (a b e) -> q a b e", a=D // 2, e=2)
+                    if x == 0:
+                        lam = lamp.tile([P, K], F32, name="lam", tag="lam")
+                        lams.append(lam)
+                        lamv = lam[:].rearrange("q (u a g l) -> q u a g l", u=UNITS, a=DQ, g=GU, l=DL)
+                    waiting = []
+                    for dq in range(DQ):
+                        pp = bank([P, DL, P], F32, "pp")
+                        for i in range(DL):
+                            d = DL * dq + i
+                            nc.tensor.matmul(out=pp[:, i, :], lhsT=ltb[:, d // 2, :, d % 2], rhs=io_sb[:],
+                                             start=True, stop=False)
+                            nc.tensor.matmul(out=pp[:, i, :], lhsT=ident_b[:, d:d + 1].to_broadcast([P, P]),
+                                             rhs=bias_sb[:, x, :], start=False, stop=True)
+                        ppv = pp[:].rearrange("q l (u g) -> q u g l", u=UNITS)
+                        if x == 0:
+                            nc.scalar.activation(out=lamv[:, :, dq, :, :], in_=ppv, func=ACT.Exp)
+                        else:
+                            kt = ktp.tile([P, DL, P], I32, name="kt", tag="kt")
+                            nc.vector.tensor_scalar(out=kt[:], in0=pp[:], scalar1=1.0 / TWO_PI, scalar2=None, op0=ALU.mult)
+                            waiting.append((dq, kt, ppv))
+                            last = dq == DQ - 1
+                            if last or len(waiting) == 2:
+                                for dw, kw, pw in (waiting if last else waiting[0:1]):
+                                    nc.vector.scalar_tensor_tensor(out=polp[:, bt, :, dw, :, :],
+                                                                   in0=kw[:].rearrange("q l (u g) -> q u g l", u=UNITS),
+                                                                   scalar=-TWO_PI, in1=pw, op0=ALU.mult, op1=ALU.add)
+                                waiting = waiting[1:]
+
+            imb_ps = bank([P, P], BF16, "imb_ps")
+            nc.tensor.transpose(imb_ps[:], imb_rows[:], ident_b[:])
+            nc.vector.tensor_copy(out=imb_col[:], in_=imb_ps[:, 0:UNITS * DQ])
+            nc.vector.tensor_reduce(out=lmask[:], in_=ident_f[:].rearrange("q (g l) -> q l g", l=DL), axis=AX.X, op=ALU.add)
+            nc.vector.tensor_tensor(out=lnsel[:], in0=lnw[:, :, 0:D].rearrange("q k (a l) -> q k a l", l=DL),
+                                    in1=lmask[:].unsqueeze(1).unsqueeze(1).to_broadcast([P, 4, DQ, DL]), op=ALU.mult)
+            nc.vector.tensor_reduce(out=lncol[:], in_=lnsel[:], axis=AX.X, op=ALU.add)
+            nc.vector.tensor_scalar(out=negw[:], in0=lncol[:, 0:4:2, :], scalar1=-1.0, scalar2=None, op0=ALU.mult)
+
+            PIECE = 1024
+            for c0 in range(0, K, PIECE):
+                cs = slice(c0, c0 + PIECE)
+                for bt in range(2):
+                    nc.scalar.activation(out=pol[:, 2 + bt, cs], in_=pol[:, bt, cs], func=ACT.Sin)
+                    nc.scalar.activation(out=pol[:, bt, cs], in_=pol[:, bt, cs], func=ACT.Abs)
+                    nc.scalar.activation(out=pol[:, bt, cs], in_=pol[:, bt, cs], func=ACT.Sin, scale=-1.0,
+                                         bias=math.pi / 2.0)
+                    nc.vector.tensor_tensor(out=pol[:, bt, cs], in0=pol[:, bt, cs], in1=lams[bt][:, cs], op=ALU.mult)
+                    nc.vector.tensor_tensor(out=pol[:, 2 + bt, cs], in0=pol[:, 2 + bt, cs], in1=lams[bt][:, cs], op=ALU.mult)
+
+        atp = ctx.enter_context(tc.tile_pool(name="atp", bufs=4))
+        xtp = ctx.enter_context(tc.tile_pool(name="xtp", bufs=10))
+        stp = ctx.enter_context(tc.tile_pool(name="stp", bufs=2))
+        rep = ctx.enter_context(tc.tile_pool(name="rep", bufs=1))
+        pcp = ctx.enter_context(tc.tile_pool(name="pcp", bufs=3))
+        yp = ctx.enter_context(tc.tile_pool(name="yp", bufs=4))
+
+        def add_up(dst, src, first, last):
+            for m in range(MT):
+                rows = slice(m * P, (m + 1) * P)
+                nc.tensor.matmul(out=dst[:, rows], lhsT=src[:, rows], rhs=ident_f[:], is_transpose=True,
+                                 start=(first and m == 0), stop=(last and m == MT - 1))
+
+        def linear_tile(a, wc, ws):
+            cols = slice(a * P, (a + 1) * P)
+            acc = bank([P, ROWS], F32, "acc")
             for g in range(PASSES):
                 nc.tensor.matmul_mx(
                     out=acc[:],
@@ -180,159 +267,97 @@ def tile_eulerinteractionlayer_pa_kernel(
                 )
             return acc
 
-        def back_tile(i, acc):
-            a_t = atp.tile([P, MT * P], F32, name="a_t", tag="a_t")
-            if i in RELU_ON_VECTOR:
-                nc.vector.tensor_scalar(out=a_t[:], in0=acc[:], scalar1=imb_col[:, i:i + 1], scalar2=0.0,
-                                        op0=ALU.add, op1=ALU.max)
-            else:
-                nc.scalar.activation(out=a_t[:], in_=acc[:], func=ACT.Relu, bias=imb_col[:, i:i + 1])
-            a4 = psum.tile([P, MT, P], F32, name="a4", tag="a4", bufs=2)
+        def sum_tile(u, a, acc):
+            i = u * DQ + a
+            a_t = atp.tile([P, ROWS], F32, name="a_t", tag="a_t")
+            nc.scalar.activation(out=a_t[:], in_=acc[:], func=ACT.Relu, bias=imb_col[:, i:i + 1])
+            pt = bank([P, ROWS], F32, "pt")
             for m in range(MT):
-                nc.tensor.transpose(a4[:, m, :], a_t[:, m * P:(m + 1) * P], ident_f[:])
-            ncols = slice(i * P, (i + 1) * P)
-            nc.vector.tensor_tensor(out=pol[:, :, ncols], in0=a4[:], in1=pol[:, :, ncols], op=ALU.add)
+                nc.tensor.transpose(pt[:, m * P:(m + 1) * P], pol[:, m, i * P:(i + 1) * P], ident_f[:])
+            x_t = xtp.tile([P, ROWS], F32, name="x_t", tag="x_t")
+            nc.vector.tensor_tensor(out=x_t[:], in0=pt[:], in1=a_t[:], op=ALU.add)
+            sq = atp.tile([P, ROWS], F32, name="sq", tag="sq")
+            nc.scalar.activation(out=sq[:], in_=x_t[:], func=ACT.Square)
+            return x_t, sq
 
-        def normalise(u, parts):
-            g0 = u * UG
-            data = [polv[:, m0:m1, g0:g0 + UG, :] for m0, m1 in parts]
-            shapes = [[P, m1 - m0, UG] for m0, m1 in parts]
-            sums = []
-            for o, shape in zip(data, shapes):
-                s1 = stp.tile(shape, F32, name="s1", tag="s1")
-                nc.vector.tensor_reduce(out=s1[:], in_=o, axis=AX.X, op=ALU.add)
-                sums.append(s1)
-            for o, shape, s1 in zip(data, shapes, sums):
-                nc.vector.scalar_tensor_tensor(out=o, in0=s1[:].unsqueeze(3).to_broadcast(shape + [D]),
-                                               scalar=-1.0 / D, in1=o, op0=ALU.mult, op1=ALU.add)
-            squares = []
-            for o, shape in zip(data, shapes):
-                sq = scr.tile(shape + [D], F32, name="sq", tag="scr")
-                nc.scalar.activation(out=sq[:], in_=o, func=ACT.Square)
-                squares.append(sq)
-            factors = []
-            for sq, shape in zip(squares, shapes):
-                s2 = stp.tile(shape, F32, name="s2", tag="s2")
-                nc.vector.tensor_reduce(out=s2[:], in_=sq[:], axis=AX.X, op=ALU.add)
-                rho = stp.tile(shape, F32, name="rho", tag="rho")
-                nc.scalar.activation(out=rho[:], in_=s2[:], func=ACT.Abs_reciprocal_sqrt, scale=1.0 / D, bias=LN_EPS)
-                factors.append(rho)
-            for o, shape, rho in zip(data, shapes, factors):
-                nc.vector.tensor_tensor(out=o, in0=o, in1=rho[:].unsqueeze(3).to_broadcast(shape + [D]), op=ALU.mult)
+        def statistics(sum1, sum2):
+            s1 = stp.tile([P, P], F32, name="s1", tag="s1")
+            nc.vector.tensor_reduce(out=s1[:], in_=sum1[:].rearrange("q (j l) -> q j l", l=DL), axis=AX.X, op=ALU.add)
+            s2 = stp.tile([P, P], F32, name="s2", tag="s2")
+            nc.vector.tensor_reduce(out=s2[:], in_=sum2[:].rearrange("q (j l) -> q j l", l=DL), axis=AX.X, op=ALU.add)
+            msq = stp.tile([P, P], F32, name="msq", tag="msq")
+            nc.scalar.activation(out=msq[:], in_=s1[:], func=ACT.Square, scale=1.0 / D)
+            var = stp.tile([P, P], F32, name="var", tag="var")
+            nc.vector.scalar_tensor_tensor(out=var[:], in0=s2[:], scalar=1.0 / D, in1=msq[:], op0=ALU.mult, op1=ALU.subtract)
+            rho = rep.tile([P, P, DL], F32, name="rho", tag="rho")
+            nc.scalar.activation(out=rho[:], in_=var[:].unsqueeze(2).to_broadcast([P, P, DL]),
+                                 func=ACT.Abs_reciprocal_sqrt, bias=LN_EPS)
+            mrho = rep.tile([P, P, DL], F32, name="mrho", tag="mrho")
+            nc.vector.scalar_tensor_tensor(out=mrho[:], in0=s1[:].unsqueeze(2).to_broadcast([P, P, DL]), scalar=1.0 / D,
+                                           in1=rho[:], op0=ALU.mult, op1=ALU.mult)
+            rho_t = stat_bank("rho_t")
+            mrho_t = stat_bank("mrho_t")
+            for dst, src in ((rho_t, rho), (mrho_t, mrho)):
+                flat = src[:].rearrange("q j l -> q (j l)")
+                for m in range(MT):
+                    nc.tensor.transpose(dst[:, m * P:(m + 1) * P], flat[:, m * P:(m + 1) * P], ident_f[:])
+            return rho_t, mrho_t
 
-        def affine_tile(i):
-            ncols = slice(i * P, (i + 1) * P)
-            t_t = psum.tile([P, MT * P], F32, name="t_t", tag="tT", bufs=1)
-            for m in range(MT):
-                nc.tensor.transpose(t_t[:, m * P:(m + 1) * P], pol[:, m, ncols], ident_f[:])
-            y_t = atp.tile([P, MT * P], F32, name="y_t", tag="y_t")
-            for rp in range(2):
-                half = slice(rp * 2 * P, (rp + 1) * 2 * P)
-                nc.scalar.activation(out=y_t[:, half], in_=t_t[:, half], func=ACT.Identity,
-                                     scale=wcol[:, i % UT, 2 * rp:2 * rp + 1],
-                                     bias=wcol[:, i % UT, 2 * rp + 1:2 * rp + 2])
-            y4 = psum.tile([P, MT, P], F32, name="y4", tag="y4", bufs=1)
-            for m in range(MT):
-                nc.tensor.transpose(y4[:, m, :], y_t[:, m * P:(m + 1) * P], ident_f[:])
-            if i in Y4_ON_VECTOR:
-                nc.vector.tensor_copy(out=pol[:, :, ncols], in_=y4[:])
-            else:
-                nc.scalar.copy(out=pol[:, :, ncols], in_=y4[:])
+        def finish(u, h, x_ts, rho_t, mrho_t):
+            if True:
+                half = slice(h * 2 * P, (h + 1) * 2 * P)
+                ys = []
+                for t in range(2):
+                    y = yp.tile([P, UC], F32, name="y", tag="y")
+                    ys.append(y)
+                for a0 in range(0, DQ, TG):
+                    banks = []
+                    for t in range(2):
+                        y_ps = bank([P, TG, P], F32, "y_ps")
+                        banks.append(y_ps)
+                    for j in range(TG):
+                        a = a0 + j
+                        pr = pcp.tile([P, 2 * P], F32, name="pr", tag="pr")
+                        nc.vector.scalar_tensor_tensor(out=pr[:], in0=x_ts[a][:, half], scalar=lncol[:, 2 * h, a:a + 1],
+                                                       in1=rho_t[:, half], op0=ALU.mult, op1=ALU.mult)
+                        sh = pcp.tile([P, 2 * P], F32, name="sh", tag="sh")
+                        nc.scalar.activation(out=sh[:], in_=mrho_t[:, half], func=ACT.Identity,
+                                             scale=negw[:, h, a:a + 1], bias=lncol[:, 2 * h + 1, a:a + 1])
+                        for t in range(2):
+                            rows = slice(t * P, (t + 1) * P)
+                            nc.tensor.matmul(out=banks[t][:, j, :], lhsT=pr[:, rows], rhs=ident_f[:], is_transpose=True,
+                                             start=True, stop=False)
+                            nc.tensor.matmul(out=banks[t][:, j, :], lhsT=sh[:, rows], rhs=ident_f[:], is_transpose=True,
+                                             start=False, stop=True)
+                    for t in range(2):
+                        dst = ys[t][:].rearrange("q (g a l) -> q g a l", g=GU, a=DQ, l=DL)[:, :, a0:a0 + TG, :]
+                        src = banks[t][:].rearrange("q a (g l) -> q g a l", l=DL)
+                        nc.vector.tensor_copy(out=dst, in_=src)
+                for t in range(2):
+                    nc.sync.dma_start(out=outv[h][:, t, u * UC:(u + 1) * UC], in_=ys[t][:])
 
-        def finish(u):
-            last_unit = u == NT // UT - 1
-            normalise(u, [(0, 2), (2, MT)] if last_unit else [(0, MT)])
-            for i in range(UT * u, UT * (u + 1)):
-                affine_tile(i)
-                if last_unit:
-                    for rp in range(2):
-                        nc.sync.dma_start(out=outv[rp][:, :, i * P:(i + 1) * P],
-                                          in_=pol[:, 2 * rp:2 * rp + 2, i * P:(i + 1) * P])
-            ucols = slice(u * UT * P, (u + 1) * UT * P)
-            if not last_unit:
-                for rp in range(2):
-                    nc.sync.dma_start(out=outv[rp][:, :, ucols], in_=pol[:, 2 * rp:2 * rp + 2, ucols])
-
-        codes = prep(0, first_w)
-
-        nc.sync.dma_start(out=io_sb[:], in_=inter_orders)
-        nc.sync.dma_start(out=bias_sb[0:D, 0, :], in_=bias_lam.rearrange("o d g -> (o d) g"))
-        nc.sync.dma_start(out=bias_sb[0:D, 1, :], in_=bias_theta.rearrange("o d g -> (o d) g"))
-        nc.sync.dma_start(out=imb_rows[0:NT, :], in_=im_b.rearrange("(i q) -> i q", q=P))
-        for k, v in enumerate((norm_r_w, norm_r_b, norm_p_w, norm_p_b)):
-            nc.sync.dma_start(out=lnw[:, k, 0:D], in_=v.partition_broadcast(P))
-
-        lsrc = [log_lam.rearrange("b f d -> b (f d)"), theta.rearrange("b f d -> b (f d)")]
-        lams = []
-        for x in range(2):
-            for bt in range(2):
-                lraw = rawp.tile([P, K], BF16, name="lraw", tag="raw")
-                nc.sync.dma_start(out=lraw[:], in_=lsrc[x][bt * P:(bt + 1) * P, :])
-                lw = lraw[:].bitcast(F32)
-                lt = ltp.tile([P, D // 2, P], F32, name="lt", tag="lt")
-                for q in range(3):
-                    tpb = psum.tile([P, 4, P], F32, name="tpb", tag="acc", bufs=4)
-                    for i in range(4):
-                        nc.tensor.transpose(tpb[:, i, :], lw[:, 4 * q + i:K // 2:D // 2], ident_f[:])
-                    nc.scalar.copy(out=lt[:, 4 * q:4 * q + 4, :], in_=tpb[:])
-                ltb = lt[:].rearrange("q a b -> q (a b)").bitcast(BF16).rearrange("q (a b e) -> q a b e", a=D // 2, e=2)
-                if x == 0:
-                    lam = scr.tile([P, F, D], F32, name="lam", tag="scr")
-                    lams.append(lam)
-                waiting = []
-                for dq in range(D // 4):
-                    pp = psum.tile([P, 4, P], F32, name="pp", tag="a4", bufs=2)
-                    for i in range(4):
-                        d = 4 * dq + i
-                        nc.tensor.matmul(out=pp[:, i, :], lhsT=ltb[:, d // 2, :, d % 2], rhs=io_sb[:],
-                                         start=True, stop=False)
-                        nc.tensor.matmul(out=pp[:, i, :], lhsT=ident_b[:, d:d + 1].to_broadcast([P, P]),
-                                         rhs=bias_sb[:, x, :], start=False, stop=True)
-                    ppv = pp[:].rearrange("q i g -> q g i")
-                    if x == 0:
-                        nc.scalar.activation(out=lam[:, :, 4 * dq:4 * dq + 4], in_=ppv, func=ACT.Exp)
-                    else:
-                        kt = ktp.tile([P, 4, P], I32, name="kt", tag="kt")
-                        nc.vector.tensor_scalar(out=kt[:], in0=pp[:], scalar1=1.0 / TWO_PI, scalar2=None, op0=ALU.mult)
-                        waiting.append((dq, kt, ppv))
-                        last = dq == D // 4 - 1
-                        if last or len(waiting) == 2:
-                            for dw, kw, pw in (waiting if last else waiting[0:1]):
-                                nc.vector.scalar_tensor_tensor(out=polv[:, bt, :, 4 * dw:4 * dw + 4],
-                                                               in0=kw[:].rearrange("q i g -> q g i"), scalar=-TWO_PI,
-                                                               in1=pw, op0=ALU.mult, op1=ALU.add)
-                            waiting = waiting[1:]
-
-        imb_ps = psum.tile([P, P], BF16, name="imb_ps", tag="tT", bufs=1)
-        nc.tensor.transpose(imb_ps[:], imb_rows[:], ident_b[:])
-        nc.vector.tensor_copy(out=imb_col[:], in_=imb_ps[:, 0:NT])
-        wfull = scr.tile([P, 4, UG, D], F32, name="wfull", tag="scr")
-        nc.vector.tensor_copy(out=wfull[:], in_=lnw[:, :, 0:D].unsqueeze(2).to_broadcast([P, 4, UG, D]))
-        wflat = wfull[:].rearrange("q k g d -> q k (g d)")
-        for i3 in range(UT):
-            wps = psum.tile([P, 4, P], F32, name="wps", tag="y4", bufs=1)
-            for k in range(4):
-                nc.tensor.transpose(wps[:, k, :], wflat[:, k, i3 * P:(i3 + 1) * P], ident_f[:])
-            nc.vector.tensor_copy(out=wcol[:, i3, :], in_=wps[:, :, 0])
-
-        PIECE = 1024
-        for c0 in range(0, K, PIECE):
-            cs = slice(c0, c0 + PIECE)
-            for bt in range(2):
-                nc.scalar.activation(out=pol[:, 2 + bt, cs], in_=pol[:, bt, cs], func=ACT.Sin)
-                nc.scalar.activation(out=pol[:, bt, cs], in_=pol[:, bt, cs], func=ACT.Abs)
-                nc.scalar.activation(out=pol[:, bt, cs], in_=pol[:, bt, cs], func=ACT.Sin, scale=-1.0,
-                                     bias=math.pi / 2.0)
-                lamf = lams[bt][:].rearrange("q g d -> q (g d)")
-                nc.vector.tensor_tensor(out=pol[:, bt, cs], in0=pol[:, bt, cs], in1=lamf[:, cs], op=ALU.mult)
-                nc.vector.tensor_tensor(out=pol[:, 2 + bt, cs], in0=pol[:, 2 + bt, cs], in1=lamf[:, cs], op=ALU.mult)
-
-        for j in range(CHUNKS):
-            nxt = prep(j + 1, None) if j + 1 < CHUNKS else None
-            tiles = range(j * (NC // P), (j + 1) * (NC // P))
-            accs = [linear_tile(i, codes[0], codes[1]) for i in tiles]
-            for i in tiles:
-                back_tile(i, accs[i % (NC // P)])
-                if i % UT == UT - 1:
-                    finish(i // UT)
+        for u in range(UNITS):
+            nxt = prep_start() if u + 1 < UNITS else None
+            sum1 = stat_bank("sum1")
+            sum2 = stat_bank("sum2")
+            x_ts = []
+            sqs = []
+            for g in range(PASSES):
+                if g < 3:
+                    pair = (2 * g, 2 * g + 1)
+                    accs = [linear_tile(a, codes[0], codes[1]) for a in pair]
+                    for a, acc in zip(pair, accs):
+                        x_t, sq = sum_tile(u, a, acc)
+                        x_ts.append(x_t)
+                        sqs.append(sq)
+                if 1 <= g <= 3:
+                    for a in (2 * g - 2, 2 * g - 1):
+                        add_up(sum1, x_ts[a], a == 0, a == DQ - 1)
+                        add_up(sum2, sqs[a], a == 0, a == DQ - 1)
+                if g == 3:
+                    rho_t, mrho_t = statistics(sum1, sum2)
+                if g >= 4:
+                    finish(u, g - 4, x_ts, rho_t, mrho_t)
+                if nxt:
+                    prep_pass(nxt, g, load_w(u + 1, g))
             codes = nxt

@@ -29,6 +29,7 @@ UC = GU * D
 DL = P // GU
 DQ = D // DL
 TG = 3
+EARLY = 4
 TWO_PI = 2.0 * math.pi
 V_WIDENS = (0, 2, 4, 5)
 
@@ -255,16 +256,19 @@ def tile_eulerinteractionlayer_pa_kernel(
                 nc.tensor.matmul(out=dst[:, rows], lhsT=src[:, rows], rhs=ident_f[:], is_transpose=True,
                                  start=(first and m == 0), stop=(last and m == MT - 1))
 
-        def linear_tile(a, wc, ws):
+        def linear_pass(acc, a, g, wc, ws):
             cols = slice(a * P, (a + 1) * P)
+            nc.tensor.matmul_mx(
+                out=acc[:],
+                lhsT=wc[:, g, cols].bitcast(FP8X4), lhsT_scale=ws[:, g, cols],
+                rhs=xc[:, g, :].bitcast(FP8X4), rhs_scale=xs[:, g, :],
+                start=(g == 0), stop=(g == PASSES - 1),
+            )
+
+        def linear_tile(a, wc, ws):
             acc = bank([P, ROWS], F32, "acc")
             for g in range(PASSES):
-                nc.tensor.matmul_mx(
-                    out=acc[:],
-                    lhsT=wc[:, g, cols].bitcast(FP8X4), lhsT_scale=ws[:, g, cols],
-                    rhs=xc[:, g, :].bitcast(FP8X4), rhs_scale=xs[:, g, :],
-                    start=(g == 0), stop=(g == PASSES - 1),
-                )
+                linear_pass(acc, a, g, wc, ws)
             return acc
 
         def sum_tile(u, a, acc):
@@ -336,18 +340,23 @@ def tile_eulerinteractionlayer_pa_kernel(
                 for t in range(2):
                     nc.sync.dma_start(out=outv[h][:, t, u * UC:(u + 1) * UC], in_=ys[t][:])
 
+        early = []
         for u in range(UNITS):
             nxt = prep_start() if u + 1 < UNITS else None
             sum1 = stat_bank("sum1")
             sum2 = stat_bank("sum2")
             x_ts = []
             sqs = []
+            accs = early
+            early = []
             for g in range(PASSES):
                 if g < 3:
                     pair = (2 * g, 2 * g + 1)
-                    accs = [linear_tile(a, codes[0], codes[1]) for a in pair]
-                    for a, acc in zip(pair, accs):
-                        x_t, sq = sum_tile(u, a, acc)
+                    for a in pair:
+                        if a >= len(accs):
+                            accs.append(linear_tile(a, codes[0], codes[1]))
+                    for a in pair:
+                        x_t, sq = sum_tile(u, a, accs[a])
                         x_ts.append(x_t)
                         sqs.append(sq)
                 if 1 <= g <= 3:
@@ -360,4 +369,11 @@ def tile_eulerinteractionlayer_pa_kernel(
                     finish(u, g - 4, x_ts, rho_t, mrho_t)
                 if nxt:
                     prep_pass(nxt, g, load_w(u + 1, g))
+                    if g == 3:
+                        for a in range(EARLY):
+                            acc = bank([P, ROWS], F32, "acc")
+                            early.append(acc)
+                    for gq in {3: (0, 1, 2), 4: (3,), 5: (4, 5)}.get(g, ()):
+                        for a in range(EARLY):
+                            linear_pass(early[a], a, gq, nxt[0], nxt[1])
             codes = nxt

@@ -114,26 +114,37 @@ def tile_eulerinteractionlayer_pa_kernel(
             state[2] = grp
 
         with ExitStack() as head:
-            rawp = head.enter_context(tc.tile_pool(name="rawp", bufs=3))
+            rawp = head.enter_context(tc.tile_pool(name="rawp", bufs=6))
             xgp = head.enter_context(tc.tile_pool(name="xgp", bufs=2))
             ltp = head.enter_context(tc.tile_pool(name="ltp", bufs=2))
             ktp = head.enter_context(tc.tile_pool(name="ktp", bufs=2))
-            lamp = head.enter_context(tc.tile_pool(name="lamp", bufs=2))
+            snp = head.enter_context(tc.tile_pool(name="snp", bufs=2))
+
+            nc.vector.memset(bias_sb[:], 0.0)
+            nc.vector.memset(imb_rows[:], 0.0)
 
             nc.sync.dma_start(out=wsc[:], in_=im_w_scale.rearrange("(g q t) o -> q g (t o)", q=P, t=4))
             first_w = []
             xraws = []
             for g in range(PASSES):
                 first_w.append(load_w(0, g))
-                if g < 3:
+                if g < MT:
                     xraw = rawp.tile([P, K], BF16, name="xraw", tag="raw")
                     nc.sync.dma_start(out=xraw[:], in_=xsrc[g])
                     xraws.append(xraw)
+            nc.sync.dma_start(out=io_sb[:], in_=inter_orders)
+            nc.sync.dma_start(out=bias_sb[0:D, 0, :], in_=bias_lam.rearrange("o d g -> (o d) g"))
+            nc.sync.dma_start(out=bias_sb[0:D, 1, :], in_=bias_theta.rearrange("o d g -> (o d) g"))
+            lsrc = [log_lam.rearrange("b f d -> b (f d)"), theta.rearrange("b f d -> b (f d)")]
+            lraws = []
+            for x in range(2):
+                for bt in range(2):
+                    lraw = rawp.tile([P, K], BF16, name="lraw", tag="raw")
+                    nc.sync.dma_start(out=lraw[:], in_=lsrc[x][bt * P:(bt + 1) * P, :])
+                    lraws.append(lraw)
 
             make_identity(nc, ident_f[:])
             make_identity(nc, ident_b[:])
-            nc.vector.memset(bias_sb[:], 0.0)
-            nc.vector.memset(imb_rows[:], 0.0)
 
             def quantise_x(m, h, xg):
                 for gi in range(2):
@@ -146,12 +157,7 @@ def tile_eulerinteractionlayer_pa_kernel(
 
             held = None
             for m in range(MT):
-                if m < 3:
-                    xraw = xraws[m]
-                else:
-                    xraw = rawp.tile([P, K], BF16, name="xraw", tag="raw")
-                    nc.sync.dma_start(out=xraw[:], in_=xsrc[m])
-                words = xraw[:].bitcast(F32)
+                words = xraws[m][:].bitcast(F32)
                 for h in range(PASSES // 2):
                     xt = bank([P, 2, 2, P], F32, "xt")
                     for gi in range(2):
@@ -169,25 +175,20 @@ def tile_eulerinteractionlayer_pa_kernel(
             quantise_x(held[0], held[1], held[2])
 
             codes = prep_start()
+            raws = []
             for g in range(PASSES):
                 prep_pass(codes, g, first_w[g])
+                raws.append(load_w(1, g))
 
-            nc.sync.dma_start(out=io_sb[:], in_=inter_orders)
-            nc.sync.dma_start(out=bias_sb[0:D, 0, :], in_=bias_lam.rearrange("o d g -> (o d) g"))
-            nc.sync.dma_start(out=bias_sb[0:D, 1, :], in_=bias_theta.rearrange("o d g -> (o d) g"))
             imbv = im_b.rearrange("(u g a l) -> u a g l", u=UNITS, g=GU, a=DQ, l=DL)
             for u in range(UNITS):
                 nc.sync.dma_start(out=imb_rows[u * DQ:(u + 1) * DQ, :].rearrange("a (g l) -> a g l", l=DL), in_=imbv[u])
             for k, v in enumerate((norm_r_w, norm_r_b, norm_p_w, norm_p_b)):
                 nc.sync.dma_start(out=lnw[:, k, 0:D], in_=v.partition_broadcast(P))
 
-            lsrc = [log_lam.rearrange("b f d -> b (f d)"), theta.rearrange("b f d -> b (f d)")]
-            lams = []
             for x in range(2):
                 for bt in range(2):
-                    lraw = rawp.tile([P, K], BF16, name="lraw", tag="raw")
-                    nc.sync.dma_start(out=lraw[:], in_=lsrc[x][bt * P:(bt + 1) * P, :])
-                    lw = lraw[:].bitcast(F32)
+                    lw = lraws[2 * x + bt][:].bitcast(F32)
                     lt = ltp.tile([P, D // 2, P], F32, name="lt", tag="lt")
                     for q in range(3):
                         tpb = bank([P, 4, P], F32, "tpb")
@@ -195,10 +196,6 @@ def tile_eulerinteractionlayer_pa_kernel(
                             nc.tensor.transpose(tpb[:, i, :], lw[:, 4 * q + i:K // 2:D // 2], ident_f[:])
                         nc.scalar.copy(out=lt[:, 4 * q:4 * q + 4, :], in_=tpb[:])
                     ltb = lt[:].rearrange("q a b -> q (a b)").bitcast(BF16).rearrange("q (a b e) -> q a b e", a=D // 2, e=2)
-                    if x == 0:
-                        lam = lamp.tile([P, K], F32, name="lam", tag="lam")
-                        lams.append(lam)
-                        lamv = lam[:].rearrange("q (u a g l) -> q u a g l", u=UNITS, a=DQ, g=GU, l=DL)
                     waiting = []
                     for dq in range(DQ):
                         pp = bank([P, DL, P], F32, "pp")
@@ -210,7 +207,7 @@ def tile_eulerinteractionlayer_pa_kernel(
                                              rhs=bias_sb[:, x, :], start=False, stop=True)
                         ppv = pp[:].rearrange("q l (u g) -> q u g l", u=UNITS)
                         if x == 0:
-                            nc.scalar.activation(out=lamv[:, :, dq, :, :], in_=ppv, func=ACT.Exp)
+                            nc.scalar.activation(out=polp[:, 2 + bt, :, dq, :, :], in_=ppv, func=ACT.Exp)
                         else:
                             kt = ktp.tile([P, DL, P], I32, name="kt", tag="kt")
                             nc.vector.tensor_scalar(out=kt[:], in0=pp[:], scalar1=1.0 / TWO_PI, scalar2=None, op0=ALU.mult)
@@ -236,12 +233,13 @@ def tile_eulerinteractionlayer_pa_kernel(
             for c0 in range(0, K, PIECE):
                 cs = slice(c0, c0 + PIECE)
                 for bt in range(2):
-                    nc.scalar.activation(out=pol[:, 2 + bt, cs], in_=pol[:, bt, cs], func=ACT.Sin)
+                    sn = snp.tile([P, PIECE], F32, name="sn", tag="sn")
+                    nc.scalar.activation(out=sn[:], in_=pol[:, bt, cs], func=ACT.Sin)
                     nc.scalar.activation(out=pol[:, bt, cs], in_=pol[:, bt, cs], func=ACT.Abs)
                     nc.scalar.activation(out=pol[:, bt, cs], in_=pol[:, bt, cs], func=ACT.Sin, scale=-1.0,
                                          bias=math.pi / 2.0)
-                    nc.vector.tensor_tensor(out=pol[:, bt, cs], in0=pol[:, bt, cs], in1=lams[bt][:, cs], op=ALU.mult)
-                    nc.vector.tensor_tensor(out=pol[:, 2 + bt, cs], in0=pol[:, 2 + bt, cs], in1=lams[bt][:, cs], op=ALU.mult)
+                    nc.vector.tensor_tensor(out=pol[:, bt, cs], in0=pol[:, bt, cs], in1=pol[:, 2 + bt, cs], op=ALU.mult)
+                    nc.vector.tensor_tensor(out=pol[:, 2 + bt, cs], in0=pol[:, 2 + bt, cs], in1=sn[:], op=ALU.mult)
 
         atp = ctx.enter_context(tc.tile_pool(name="atp", bufs=4))
         xtp = ctx.enter_context(tc.tile_pool(name="xtp", bufs=10))
@@ -336,7 +334,10 @@ def tile_eulerinteractionlayer_pa_kernel(
                     for t in range(2):
                         dst = ys[t][:].rearrange("q (g a l) -> q g a l", g=GU, a=DQ, l=DL)[:, :, a0:a0 + TG, :]
                         src = banks[t][:].rearrange("q a (g l) -> q g a l", l=DL)
-                        nc.vector.tensor_copy(out=dst, in_=src)
+                        if t == 0:
+                            nc.vector.tensor_copy(out=dst, in_=src)
+                        else:
+                            nc.scalar.copy(out=dst, in_=src)
                 for t in range(2):
                     nc.sync.dma_start(out=outv[h][:, t, u * UC:(u + 1) * UC], in_=ys[t][:])
 
@@ -368,7 +369,9 @@ def tile_eulerinteractionlayer_pa_kernel(
                 if g >= 4:
                     finish(u, g - 4, x_ts, rho_t, mrho_t)
                 if nxt:
-                    prep_pass(nxt, g, load_w(u + 1, g))
+                    prep_pass(nxt, g, raws[g])
+                    if u + 2 < UNITS:
+                        raws[g] = load_w(u + 2, g)
                     if g == 3:
                         for a in range(EARLY):
                             acc = bank([P, ROWS], F32, "acc")

@@ -245,7 +245,7 @@ def tile_eulerinteractionlayer_pa_kernel(
         xtp = ctx.enter_context(tc.tile_pool(name="xtp", bufs=10))
         stp = ctx.enter_context(tc.tile_pool(name="stp", bufs=2))
         rep = ctx.enter_context(tc.tile_pool(name="rep", bufs=1))
-        pcp = ctx.enter_context(tc.tile_pool(name="pcp", bufs=3))
+        pcp = ctx.enter_context(tc.tile_pool(name="pcp", bufs=6))
         yp = ctx.enter_context(tc.tile_pool(name="yp", bufs=4))
 
         def add_up(dst, src, first, last):

from contextlib import ExitStack
import math

import concourse.mybir as mybir
from concourse.masks import make_identity

B, F, D = 256, 128, 24
K = F * D
LN_EPS = 1e-5

F32 = mybir.dt.float32
BF16 = mybir.dt.bfloat16
I32 = mybir.dt.int32
U32 = mybir.dt.uint32
U8 = mybir.dt.uint8
FP8 = mybir.dt.float8_e4m3fn
FP8X4 = mybir.dt.float8_e4m3fn_x4
ALU = mybir.AluOpType
ACT = mybir.ActivationFunctionType
AX = mybir.AxisListType

P = 128
PASSES = K // 512
MT = 4
ROWS = MT * P
UNITS = 4
GU = F // UNITS
UC = GU * D
DL = P // GU
DQ = D // DL
TG = 3
EARLY = 4
TWO_PI = 2.0 * math.pi
V_WIDENS = (0, 2, 4, 5)

FLOPS = 2 * (2 * B) * K * K + 2 * 2 * B * D * F * F


def tile_eulerinteractionlayer_pa_kernel(
    tc, r, p, log_lam, theta, inter_orders, im_w_bytes, im_w_scale, im_b,
    bias_lam, bias_theta, norm_r_w, norm_r_b, norm_p_w, norm_p_b, out_0, out_1,
):
    nc = tc.nc
    with ExitStack() as ctx:
        const = ctx.enter_context(tc.tile_pool(name="const", bufs=1))
        wrawp = ctx.enter_context(tc.tile_pool(name="wrawp", bufs=6))
        plp = ctx.enter_context(tc.tile_pool(name="plp", bufs=3))
        grp_pool = ctx.enter_context(tc.tile_pool(name="grpp", bufs=3))
        wcp = ctx.enter_context(tc.tile_pool(name="wcp", bufs=2))
        psum = ctx.enter_context(tc.psum_pool(name="psum", bufs=2))

        def bank(shape, dtype, name):
            return psum.tile(shape, dtype, name=name, tag="ring", bufs=6)

        def stat_bank(name):
            return psum.tile([P, ROWS], F32, name=name, tag="stat", bufs=2)

        wview = im_w_bytes.rearrange("(g q t) n -> g q t n", q=P, t=4)
        outv = [o.rearrange("(t q) g d -> q t (g d)", q=P) for o in (out_0, out_1)]
        r2 = r.rearrange("b f d -> b (f d)")
        p2 = p.rearrange("b f d -> b (f d)")
        xsrc = [r2[0:P, :], r2[P:2 * P, :], p2[0:P, :], p2[P:2 * P, :]]

        def load_w(u, g):
            wraw = wrawp.tile([P, 4, UC], U8, name="wraw", tag="wraw")
            nc.sync.dma_start(out=wraw[:], in_=wview[g][:, :, u * UC:(u + 1) * UC])
            return wraw

        wsc = const.tile([P, PASSES, 4], F32, name="wsc")
        ident_f = const.tile([P, P], F32, name="ident_f")
        ident_b = const.tile([P, P], BF16, name="ident_b")
        io_sb = const.tile([P, P], BF16, name="io_sb")
        bias_sb = const.tile([P, 2, P], BF16, name="bias_sb")
        imb_rows = const.tile([P, P], BF16, name="imb_rows")
        imb_col = const.tile([P, UNITS * DQ], F32, name="imb_col")
        lnw = const.tile([P, 4, 32], BF16, name="lnw")
        lmask = const.tile([P, DL], F32, name="lmask")
        lnsel = const.tile([P, 4, DQ, DL], F32, name="lnsel")
        lncol = const.tile([P, 4, DQ], F32, name="lncol")
        negw = const.tile([P, 2, DQ], F32, name="negw")
        xc = const.tile([P, PASSES, ROWS], U32, name="xc", align_bytes=64)
        xs = const.tile([P, PASSES, ROWS], U8, name="xs", align_bytes=64)
        pol = const.tile([P, MT, K], F32, name="pol")
        polp = pol[:].rearrange("q m (u a g l) -> q m u a g l", u=UNITS, a=DQ, g=GU, l=DL)

        def quantise_w(wc, ws, g, grp):
            flat = grp[:].rearrange("q c t -> q (c t)")
            for c0, c1 in ((0, 512), (512, UC)):
                nc.vector.quantize_mx(out=wc[:, g, c0:c1].bitcast(FP8X4), scales=ws[:, g, c0:c1],
                                      in_=flat[:, 4 * c0:4 * c1])

        def prep_start():
            wc = wcp.tile([P, PASSES, UC], U32, name="wc", tag="wc", align_bytes=64)
            ws = wcp.tile([P, PASSES, UC], U8, name="ws", tag="ws", align_bytes=64)
            return [wc, ws, None]

        def prep_pass(state, g, wraw):
            wc, ws, waiting = state
            planes = plp.tile([P, 4, UC], BF16, name="planes", tag="planes")
            for t in range(4):
                if t == 3 and g in V_WIDENS:
                    nc.vector.tensor_scalar(out=planes[:, t, :], in0=wraw[:, t, :].bitcast(FP8),
                                            scalar1=wsc[:, g, t:t + 1], scalar2=None, op0=ALU.mult)
                else:
                    nc.scalar.activation(out=planes[:, t, :], in_=wraw[:, t, :].bitcast(FP8), func=ACT.Copy,
                                         scale=wsc[:, g, t:t + 1])
            grp = grp_pool.tile([P, UC, 4], BF16, name="grp", tag="grp", align_bytes=64)
            nc.vector.tensor_copy(out=grp[:].rearrange("q (a g l) t -> q g a l t", a=DQ, g=GU, l=DL),
                                  in_=planes[:].rearrange("q t (g a l) -> q g a l t", g=GU, a=DQ, l=DL))
            if waiting:
                quantise_w(wc, ws, g - 1, waiting)
            if g == PASSES - 1:
                quantise_w(wc, ws, g, grp)
            state[2] = grp

        with ExitStack() as head:
            rawp = head.enter_context(tc.tile_pool(name="rawp", bufs=6))
            xgp = head.enter_context(tc.tile_pool(name="xgp", bufs=2))
            ltp = head.enter_context(tc.tile_pool(name="ltp", bufs=2))
            ktp = head.enter_context(tc.tile_pool(name="ktp", bufs=2))
            snp = head.enter_context(tc.tile_pool(name="snp", bufs=2))

            nc.vector.memset(bias_sb[:], 0.0)
            nc.vector.memset(imb_rows[:], 0.0)

            nc.sync.dma_start(out=wsc[:], in_=im_w_scale.rearrange("(g q t) o -> q g (t o)", q=P, t=4))
            first_w = []
            xraws = []
            for g in range(PASSES):
                first_w.append(load_w(0, g))
                if g < MT:
                    xraw = rawp.tile([P, K], BF16, name="xraw", tag="raw")
                    nc.sync.dma_start(out=xraw[:], in_=xsrc[g])
                    xraws.append(xraw)
            nc.sync.dma_start(out=io_sb[:], in_=inter_orders)
            nc.sync.dma_start(out=bias_sb[0:D, 0, :], in_=bias_lam.rearrange("o d g -> (o d) g"))
            nc.sync.dma_start(out=bias_sb[0:D, 1, :], in_=bias_theta.rearrange("o d g -> (o d) g"))
            lsrc = [log_lam.rearrange("b f d -> b (f d)"), theta.rearrange("b f d -> b (f d)")]
            lraws = []
            for x in range(2):
                for bt in range(2):
                    lraw = rawp.tile([P, K], BF16, name="lraw", tag="raw")
                    nc.sync.dma_start(out=lraw[:], in_=lsrc[x][bt * P:(bt + 1) * P, :])
                    lraws.append(lraw)

            make_identity(nc, ident_f[:])
            make_identity(nc, ident_b[:])

            def quantise_x(m, h, xg):
                for gi in range(2):
                    g = 2 * h + gi
                    nc.vector.quantize_mx(
                        out=xc[:, g, m * P:(m + 1) * P].bitcast(FP8X4),
                        scales=xs[:, g, m * P:(m + 1) * P],
                        in_=xg[:, gi, :, :].rearrange("q r t -> q (r t)"),
                    )

            held = None
            for m in range(MT):
                words = xraws[m][:].bitcast(F32)
                for h in range(PASSES // 2):
                    xt = bank([P, 2, 2, P], F32, "xt")
                    for gi in range(2):
                        g = 2 * h + gi
                        for w in range(2):
                            nc.tensor.transpose(xt[:, gi, w, :], words[:, 256 * g + w:256 * (g + 1):2], ident_f[:])
                    xg = xgp.tile([P, 2, P, 4], BF16, name="xg", tag="xg", align_bytes=64)
                    nc.vector.tensor_copy(
                        out=xg[:].rearrange("q a r t -> q (a r t)").bitcast(F32).rearrange("q (a r w) -> q a r w", a=2, w=2),
                        in_=xt[:].rearrange("q a w r -> q a r w"),
                    )
                    if held:
                        quantise_x(held[0], held[1], held[2])
                    held = (m, h, xg)
            quantise_x(held[0], held[1], held[2])

            codes = prep_start()
            raws = []
            for g in range(PASSES):
                prep_pass(codes, g, first_w[g])
                raws.append(load_w(1, g))

            imbv = im_b.rearrange("(u g a l) -> u a g l", u=UNITS, g=GU, a=DQ, l=DL)
            for u in range(UNITS):
                nc.sync.dma_start(out=imb_rows[u * DQ:(u + 1) * DQ, :].rearrange("a (g l) -> a g l", l=DL), in_=imbv[u])
            for k, v in enumerate((norm_r_w, norm_r_b, norm_p_w, norm_p_b)):
                nc.sync.dma_start(out=lnw[:, k, 0:D], in_=v.partition_broadcast(P))

            for x in range(2):
                for bt in range(2):
                    lw = lraws[2 * x + bt][:].bitcast(F32)
                    lt = ltp.tile([P, D // 2, P], F32, name="lt", tag="lt")
                    for q in range(3):
                        tpb = bank([P, 4, P], F32, "tpb")
                        for i in range(4):
                            nc.tensor.transpose(tpb[:, i, :], lw[:, 4 * q + i:K // 2:D // 2], ident_f[:])
                        nc.scalar.copy(out=lt[:, 4 * q:4 * q + 4, :], in_=tpb[:])
                    ltb = lt[:].rearrange("q a b -> q (a b)").bitcast(BF16).rearrange("q (a b e) -> q a b e", a=D // 2, e=2)
                    waiting = []
                    for dq in range(DQ):
                        pp = bank([P, DL, P], F32, "pp")
                        for i in range(DL):
                            d = DL * dq + i
                            nc.tensor.matmul(out=pp[:, i, :], lhsT=ltb[:, d // 2, :, d % 2], rhs=io_sb[:],
                                             start=True, stop=False)
                            nc.tensor.matmul(out=pp[:, i, :], lhsT=ident_b[:, d:d + 1].to_broadcast([P, P]),
                                             rhs=bias_sb[:, x, :], start=False, stop=True)
                        ppv = pp[:].rearrange("q l (u g) -> q u g l", u=UNITS)
                        if x == 0:
                            nc.scalar.activation(out=polp[:, 2 + bt, :, dq, :, :], in_=ppv, func=ACT.Exp)
                        else:
                            kt = ktp.tile([P, DL, P], I32, name="kt", tag="kt")
                            nc.vector.tensor_scalar(out=kt[:], in0=pp[:], scalar1=1.0 / TWO_PI, scalar2=None, op0=ALU.mult)
                            waiting.append((dq, kt, ppv))
                            last = dq == DQ - 1
                            if last or len(waiting) == 2:
                                for dw, kw, pw in (waiting if last else waiting[0:1]):
                                    nc.vector.scalar_tensor_tensor(out=polp[:, bt, :, dw, :, :],
                                                                   in0=kw[:].rearrange("q l (u g) -> q u g l", u=UNITS),
                                                                   scalar=-TWO_PI, in1=pw, op0=ALU.mult, op1=ALU.add)
                                waiting = waiting[1:]

            imb_ps = bank([P, P], BF16, "imb_ps")
            nc.tensor.transpose(imb_ps[:], imb_rows[:], ident_b[:])
            nc.vector.tensor_copy(out=imb_col[:], in_=imb_ps[:, 0:UNITS * DQ])
            nc.vector.tensor_reduce(out=lmask[:], in_=ident_f[:].rearrange("q (g l) -> q l g", l=DL), axis=AX.X, op=ALU.add)
            nc.vector.tensor_tensor(out=lnsel[:], in0=lnw[:, :, 0:D].rearrange("q k (a l) -> q k a l", l=DL),
                                    in1=lmask[:].unsqueeze(1).unsqueeze(1).to_broadcast([P, 4, DQ, DL]), op=ALU.mult)
            nc.vector.tensor_reduce(out=lncol[:], in_=lnsel[:], axis=AX.X, op=ALU.add)
            nc.vector.tensor_scalar(out=negw[:], in0=lncol[:, 0:4:2, :], scalar1=-1.0, scalar2=None, op0=ALU.mult)

            PIECE = 1024
            for c0 in range(0, K, PIECE):
                cs = slice(c0, c0 + PIECE)
                for bt in range(2):
                    sn = snp.tile([P, PIECE], F32, name="sn", tag="sn")
                    nc.scalar.activation(out=sn[:], in_=pol[:, bt, cs], func=ACT.Sin)
                    nc.scalar.activation(out=pol[:, bt, cs], in_=pol[:, bt, cs], func=ACT.Abs)
                    nc.scalar.activation(out=pol[:, bt, cs], in_=pol[:, bt, cs], func=ACT.Sin, scale=-1.0,
                                         bias=math.pi / 2.0)
                    nc.vector.tensor_tensor(out=pol[:, bt, cs], in0=pol[:, bt, cs], in1=pol[:, 2 + bt, cs], op=ALU.mult)
                    nc.vector.tensor_tensor(out=pol[:, 2 + bt, cs], in0=pol[:, 2 + bt, cs], in1=sn[:], op=ALU.mult)

        atp = ctx.enter_context(tc.tile_pool(name="atp", bufs=4))
        xtp = ctx.enter_context(tc.tile_pool(name="xtp", bufs=10))
        stp = ctx.enter_context(tc.tile_pool(name="stp", bufs=2))
        rep = ctx.enter_context(tc.tile_pool(name="rep", bufs=1))
        pcp = ctx.enter_context(tc.tile_pool(name="pcp", bufs=6))
        yp = ctx.enter_context(tc.tile_pool(name="yp", bufs=4))

        def add_up(dst, src, first, last):
            for m in range(MT):
                rows = slice(m * P, (m + 1) * P)
                nc.tensor.matmul(out=dst[:, rows], lhsT=src[:, rows], rhs=ident_f[:], is_transpose=True,
                                 start=(first and m == 0), stop=(last and m == MT - 1))

        def linear_pass(acc, a, g, wc, ws):
            cols = slice(a * P, (a + 1) * P)
            nc.tensor.matmul_mx(
                out=acc[:],
                lhsT=wc[:, g, cols].bitcast(FP8X4), lhsT_scale=ws[:, g, cols],
                rhs=xc[:, g, :].bitcast(FP8X4), rhs_scale=xs[:, g, :],
                start=(g == 0), stop=(g == PASSES - 1),
            )

        def linear_tile(a, wc, ws):
            acc = bank([P, ROWS], F32, "acc")
            for g in range(PASSES):
                linear_pass(acc, a, g, wc, ws)
            return acc

        def sum_tile(u, a, acc):
            i = u * DQ + a
            a_t = atp.tile([P, ROWS], F32, name="a_t", tag="a_t")
            nc.scalar.activation(out=a_t[:], in_=acc[:], func=ACT.Relu, bias=imb_col[:, i:i + 1])
            pt = bank([P, ROWS], F32, "pt")
            for m in range(MT):
                nc.tensor.transpose(pt[:, m * P:(m + 1) * P], pol[:, m, i * P:(i + 1) * P], ident_f[:])
            x_t = xtp.tile([P, ROWS], F32, name="x_t", tag="x_t")
            nc.vector.tensor_tensor(out=x_t[:], in0=pt[:], in1=a_t[:], op=ALU.add)
            sq = atp.tile([P, ROWS], F32, name="sq", tag="sq")
            nc.scalar.activation(out=sq[:], in_=x_t[:], func=ACT.Square)
            return x_t, sq

        def statistics(sum1, sum2):
            s1 = stp.tile([P, P], F32, name="s1", tag="s1")
            nc.vector.tensor_reduce(out=s1[:], in_=sum1[:].rearrange("q (j l) -> q j l", l=DL), axis=AX.X, op=ALU.add)
            s2 = stp.tile([P, P], F32, name="s2", tag="s2")
            nc.vector.tensor_reduce(out=s2[:], in_=sum2[:].rearrange("q (j l) -> q j l", l=DL), axis=AX.X, op=ALU.add)
            msq = stp.tile([P, P], F32, name="msq", tag="msq")
            nc.scalar.activation(out=msq[:], in_=s1[:], func=ACT.Square, scale=1.0 / D)
            var = stp.tile([P, P], F32, name="var", tag="var")
            nc.vector.scalar_tensor_tensor(out=var[:], in0=s2[:], scalar=1.0 / D, in1=msq[:], op0=ALU.mult, op1=ALU.subtract)
            rho = rep.tile([P, P, DL], F32, name="rho", tag="rho")
            nc.scalar.activation(out=rho[:], in_=var[:].unsqueeze(2).to_broadcast([P, P, DL]),
                                 func=ACT.Abs_reciprocal_sqrt, bias=LN_EPS)
            mrho = rep.tile([P, P, DL], F32, name="mrho", tag="mrho")
            nc.vector.scalar_tensor_tensor(out=mrho[:], in0=s1[:].unsqueeze(2).to_broadcast([P, P, DL]), scalar=1.0 / D,
                                           in1=rho[:], op0=ALU.mult, op1=ALU.mult)
            rho_t = stat_bank("rho_t")
            mrho_t = stat_bank("mrho_t")
            for dst, src in ((rho_t, rho), (mrho_t, mrho)):
                flat = src[:].rearrange("q j l -> q (j l)")
                for m in range(MT):
                    nc.tensor.transpose(dst[:, m * P:(m + 1) * P], flat[:, m * P:(m + 1) * P], ident_f[:])
            return rho_t, mrho_t

        def finish(u, h, x_ts, rho_t, mrho_t):
            if True:
                half = slice(h * 2 * P, (h + 1) * 2 * P)
                ys = []
                for t in range(2):
                    y = yp.tile([P, UC], F32, name="y", tag="y")
                    ys.append(y)
                for a0 in range(0, DQ, TG):
                    banks = []
                    for t in range(2):
                        y_ps = bank([P, TG, P], F32, "y_ps")
                        banks.append(y_ps)
                    for j in range(TG):
                        a = a0 + j
                        pr = pcp.tile([P, 2 * P], F32, name="pr", tag="pr")
                        nc.vector.scalar_tensor_tensor(out=pr[:], in0=x_ts[a][:, half], scalar=lncol[:, 2 * h, a:a + 1],
                                                       in1=rho_t[:, half], op0=ALU.mult, op1=ALU.mult)
                        sh = pcp.tile([P, 2 * P], F32, name="sh", tag="sh")
                        nc.scalar.activation(out=sh[:], in_=mrho_t[:, half], func=ACT.Identity,
                                             scale=negw[:, h, a:a + 1], bias=lncol[:, 2 * h + 1, a:a + 1])
                        for t in range(2):
                            rows = slice(t * P, (t + 1) * P)
                            nc.tensor.matmul(out=banks[t][:, j, :], lhsT=pr[:, rows], rhs=ident_f[:], is_transpose=True,
                                             start=True, stop=False)
                            nc.tensor.matmul(out=banks[t][:, j, :], lhsT=sh[:, rows], rhs=ident_f[:], is_transpose=True,
                                             start=False, stop=True)
                    for t in range(2):
                        dst = ys[t][:].rearrange("q (g a l) -> q g a l", g=GU, a=DQ, l=DL)[:, :, a0:a0 + TG, :]
                        src = banks[t][:].rearrange("q a (g l) -> q g a l", l=DL)
                        if t == 0:
                            nc.vector.tensor_copy(out=dst, in_=src)
                        else:
                            nc.scalar.copy(out=dst, in_=src)
                for t in range(2):
                    nc.sync.dma_start(out=outv[h][:, t, u * UC:(u + 1) * UC], in_=ys[t][:])

        early = []
        for u in range(UNITS):
            nxt = prep_start() if u + 1 < UNITS else None
            sum1 = stat_bank("sum1")
            sum2 = stat_bank("sum2")
            x_ts = []
            sqs = []
            accs = early
            early = []
            for g in range(PASSES):
                if g < 3:
                    pair = (2 * g, 2 * g + 1)
                    for a in pair:
                        if a >= len(accs):
                            accs.append(linear_tile(a, codes[0], codes[1]))
                    for a in pair:
                        x_t, sq = sum_tile(u, a, accs[a])
                        x_ts.append(x_t)
                        sqs.append(sq)
                if 1 <= g <= 3:
                    for a in (2 * g - 2, 2 * g - 1):
                        add_up(sum1, x_ts[a], a == 0, a == DQ - 1)
                        add_up(sum2, sqs[a], a == 0, a == DQ - 1)
                if g == 3:
                    rho_t, mrho_t = statistics(sum1, sum2)
                if g >= 4:
                    finish(u, g - 4, x_ts, rho_t, mrho_t)
                if nxt:
                    prep_pass(nxt, g, raws[g])
                    if u + 2 < UNITS:
                        raws[g] = load_w(u + 2, g)
                    if g == 3:
                        for a in range(EARLY):
                            acc = bank([P, ROWS], F32, "acc")
                            early.append(acc)
                    for gq in {3: (0, 1, 2), 4: (3,), 5: (4, 5)}.get(g, ()):
                        for a in range(EARLY):
                            linear_pass(early[a], a, gq, nxt[0], nxt[1])
            codes = nxt
